import numpy as np
import ml_dtypes


def mxq(x, axis, fmt="e4m3"):
    dtype, down = {"e4m3": (ml_dtypes.float8_e4m3fn, 7), "e5m2": (ml_dtypes.float8_e5m2, 14)}[fmt]
    v = np.moveaxis(np.asarray(x, np.float32).astype(ml_dtypes.bfloat16).astype(np.float64), axis, -1)
    blocks = v.reshape(v.shape[:-1] + (-1, 32))
    amax = np.abs(blocks).max(-1, keepdims=True)
    byte = np.maximum(np.where(amax > 0, np.frexp(amax)[1] - 1 + 127, 0) - down, 1)
    scale = np.exp2(byte - 127.0)
    codes = (blocks / scale).astype(np.float32).astype(dtype).astype(np.float64)
    return np.moveaxis((codes * scale).reshape(v.shape), -1, axis)


WIDE = False


def mx_kscale(k):
    if not WIDE:
        return np.ones(k)
    levels = np.array([10, -10, 5, -5, 0])
    a = np.random.permutation(np.resize(levels, k // 512 * 4)).reshape(k // 512, 4)
    idx = np.arange(k)
    return np.exp2(a[idx // 512, idx % 128 // 32])


BF16 = ml_dtypes.bfloat16


def bf(x):
    return np.asarray(x, np.float32).astype(BF16)


def f64(x):
    return np.asarray(x).astype(np.float64)


E2M1 = np.array([0.0, 0.5, 1.0, 1.5, 2.0, 3.0, 4.0, 6.0, -0.0, -0.5, -1.0, -1.5, -2.0, -3.0, -4.0, -6.0])


def pack_weight(w, fmt):
    k, n = w.shape
    w = f64(bf(w)).reshape(k // 32, 32, n)
    amax = np.abs(w).max(1)
    if fmt == "e4m3":
        byte = np.frexp(amax)[1] - 1 + 127 - 7
    else:
        mant, ex = np.frexp(amax / 6.0)
        byte = np.where(mant > 0.5, ex, ex - 1) + 127
    byte = np.clip(np.where(amax > 0, byte, 1), 1, 254)
    scaled = (w * np.exp2(127.0 - byte)[:, None, :]).reshape(k, n).astype(np.float32)
    by_word = np.ascontiguousarray(scaled.reshape(k // 512, 128, 4, n).transpose(0, 1, 3, 2))
    if fmt == "e4m3":
        words = by_word.astype(ml_dtypes.float8_e4m3fn).view(np.uint8)
    else:
        c = by_word.astype(ml_dtypes.float4_e2m1fn).view(np.uint8) & 0xF
        words = c[..., 0::2] | (c[..., 1::2] << 4)
    return np.ascontiguousarray(words), np.ascontiguousarray(byte.astype(np.uint8).reshape(k // 512, 16, n))


def unpack_weight(words, scales, fmt):
    g, p, n, _ = words.shape
    if fmt == "e4m3":
        vals = np.ascontiguousarray(words).view(ml_dtypes.float8_e4m3fn).astype(np.float64)
    else:
        nib = np.empty((g, p, n, 4), np.uint8)
        nib[..., 0::2] = words & 0xF
        nib[..., 1::2] = words >> 4
        vals = E2M1[nib]
    vals = vals * np.repeat(np.exp2(scales.astype(np.float64) - 127.0), 8, axis=1)[..., None]
    return vals.transpose(0, 1, 3, 2).reshape(g * 512, n)

def pack4(w):
    words, scales = pack_weight(w, "e2m1")
    return words.reshape(words.shape[0], 128, -1), scales


def unpack4(words, scales):
    return unpack_weight(words.reshape(words.shape[0], 128, -1, 2), scales, "e2m1")


B, N, SIZE, CH = 256, 16, 1024, 512


def sigmoid(v):
    return 1.0 / (1.0 + np.exp(-v))


def setup_inputs():
    s = mx_kscale(SIZE)
    half = np.concatenate([np.ones(CH), np.full(CH, 2.0 / np.sqrt(N))])
    z_node = bf(np.random.standard_normal((B, N, SIZE)) * s)
    z_children = bf(np.random.standard_normal((B, N, SIZE)) * half)
    w_f = np.random.standard_normal((CH, SIZE)) / np.sqrt(SIZE) / s
    words, scales = pack4(np.ascontiguousarray(w_f.T))
    U_f = bf(np.random.standard_normal((CH, CH)) / np.sqrt(CH))
    b_f = bf(np.random.standard_normal(CH) * 0.5)
    return {"z_node": z_node,
            "z_children": z_children,
            "W_f_words": words,
            "W_f_scales": scales,
            "U_f": U_f,
            "b_f": b_f}


def reference(z_node, z_children, W_f_words, W_f_scales, U_f, b_f):
    h_k = f64(z_children)[..., :CH]
    c_k = f64(z_children)[..., CH:]
    f_j_k = sigmoid((mxq(f64(z_node), 2, "e4m3") @ unpack4(W_f_words, W_f_scales)) + h_k @ f64(U_f).T + f64(b_f))
    return (f_j_k * c_k).sum(axis=1)

@@ -1,0 +1,211 @@
+from contextlib import ExitStack
+
+import concourse.mybir as mybir
+from concourse.masks import make_identity
+
+F32 = mybir.dt.float32
+BF16 = mybir.dt.bfloat16
+I32 = mybir.dt.int32
+U32 = mybir.dt.uint32
+U8 = mybir.dt.uint8
+FP8X4 = mybir.dt.float8_e4m3fn_x4
+FP4X4 = mybir.dt.float4_e2m1fn_x4
+ADD = mybir.AluOpType.add
+MULT = mybir.AluOpType.mult
+SIGMOID = mybir.ActivationFunctionType.Sigmoid
+
+P = 128
+NODES, CHILDREN, SIZE, CH = 256, 16, 1024, 512
+PASSES = SIZE // (4 * P)
+HALVES = CH // (2 * P)
+PAIR = 2
+ROUNDS_PER_BLOCK = CHILDREN // PAIR
+ROUNDS = (NODES // P) * ROUNDS_PER_BLOCK
+AHEAD = 3
+
+FLOPS = 2 * NODES * CHILDREN * CH * (SIZE + CH)
+
+
+def tile_treelstm_pa_kernel(tc, z_node, z_children, W_f_words, W_f_scales, U_f, b_f, out):
+    nc = tc.nc
+    with ExitStack() as stack:
+        consts = stack.enter_context(tc.tile_pool(name="consts", bufs=1))
+        z_pool = stack.enter_context(tc.tile_pool(name="z_pool", bufs=AHEAD + 1))
+        c_pool = stack.enter_context(tc.tile_pool(name="c_pool", bufs=AHEAD + 4))
+        work = stack.enter_context(tc.tile_pool(name="work", bufs=3))
+        totals = stack.enter_context(tc.tile_pool(name="totals", bufs=2))
+        psum_z = stack.enter_context(tc.psum_pool(name="psum_z", bufs=PAIR))
+        psum_h = stack.enter_context(tc.psum_pool(name="psum_h", bufs=1))
+        psum_plain = stack.enter_context(tc.psum_pool(name="psum_plain", bufs=PAIR))
+        psum_mx = stack.enter_context(tc.psum_pool(name="psum_mx", bufs=PAIR))
+        stack.enter_context(tc.manual_schedule())
+
+        z_tiles, c_tiles, zT_banks, hT_banks = {}, {}, {}, {}
+        grouped_tiles, hT_tiles, code_tiles, plane_tiles = {}, {}, {}, {}
+        plain_banks, mx_banks, pre_tiles, gate_tiles, total_tiles = {}, {}, {}, {}, {}
+
+        def load(r):
+            nodes = slice((r // ROUNDS_PER_BLOCK) * P, (r // ROUNDS_PER_BLOCK + 1) * P)
+            children = slice((r % ROUNDS_PER_BLOCK) * PAIR, (r % ROUNDS_PER_BLOCK + 1) * PAIR)
+            z_sb = z_pool.tile([P, PAIR, SIZE], BF16)
+            nc.sync.dma_start(out=z_sb[:], in_=z_node[nodes, children, :])
+            c_sb = c_pool.tile([P, PAIR, SIZE], BF16)
+            nc.sync.dma_start(out=c_sb[:], in_=z_children[nodes, children, :])
+            z_tiles[r], c_tiles[r] = z_sb, c_sb
+
+        ident = consts.tile([P, P], F32)
+        make_identity(nc, ident[:])
+
+        bias_row = consts.tile([P, CH], BF16)
+        nc.vector.memset(bias_row[:], 0.0)
+        nc.sync.dma_start(out=bias_row[0:1, :], in_=b_f.rearrange("(o n) -> o n", o=1))
+
+        warm = consts.tile([P, 1], F32)
+        nc.vector.memset(warm[:], 0.0)
+        nc.scalar.activation(out=warm[:], in_=warm[:], func=SIGMOID)
+
+        w_planes = consts.tile([P, PASSES, CH], U8, align_bytes=64)
+        nc.vector.memset(w_planes[:].bitcast(I32), 0)
+        ones = consts.tile([P, P], BF16)
+        nc.vector.memset(ones[:], 1.0)
+
+        u_sb = consts.tile([P, CH // P, CH], BF16)
+        nc.sync.dma_start(out=u_sb[:], in_=U_f.rearrange("(a p) k -> p a k", p=P))
+        load(0)
+        w_words = consts.tile([P, PASSES, 2 * CH], U8, align_bytes=64)
+        nc.sync.dma_start(out=w_words[:].bitcast(I32), in_=W_f_words.bitcast(I32).rearrange("g p n -> p g n"))
+        for quadrant in range(4):
+            nc.sync.dma_start(
+                out=w_planes[32 * quadrant : 32 * quadrant + 4].bitcast(I32),
+                in_=W_f_scales.bitcast(I32)[:, 4 * quadrant : 4 * quadrant + 4, :].rearrange("g q n -> q g n"),
+            )
+        for r in range(1, AHEAD):
+            load(r)
+
+        uT = consts.tile([P, HALVES, 2, CH], BF16)
+        for j in range(HALVES):
+            uT_ps = psum_z.tile([P, CH // P, P], F32, tag="zT_ps")
+            for a in range(CH // P):
+                nc.tensor.transpose(uT_ps[:, a, :], u_sb[:, a, :].bitcast(F32)[:, P * j : P * (j + 1)], ident[:])
+            pairs = uT_ps[:].rearrange("p a c -> p (a c)").bitcast(BF16).rearrange("p (c e) -> p e c", e=2)
+            nc.vector.tensor_copy(out=uT[:, j], in_=pairs)
+
+        bias_ps = psum_plain.tile([P, CH], F32, tag="plain_ps")
+        nc.tensor.matmul(out=bias_ps[:], lhsT=ones[:], rhs=bias_row[:], start=True, stop=True)
+        bias = consts.tile([P, CH], F32)
+        nc.vector.tensor_copy(out=bias[:], in_=bias_ps[:])
+
+        def transposes(r):
+            zT_banks[r] = []
+            for i in range(PAIR):
+                zT_ps = psum_z.tile([P, PASSES, 2, P], F32)
+                z_words = z_tiles[r][:, i, :].bitcast(F32)
+                for g in range(PASSES):
+                    for u in range(2):
+                        nc.tensor.transpose(zT_ps[:, g, u, :], z_words[:, 2 * P * g + u : 2 * P * (g + 1) : 2], ident[:])
+                zT_banks[r].append(zT_ps)
+            hT_ps = psum_h.tile([P, PAIR, HALVES, P], F32)
+            for i in range(PAIR):
+                h_words = c_tiles[r][:, i, 0:CH].bitcast(F32)
+                for j in range(HALVES):
+                    nc.tensor.transpose(hT_ps[:, i, j, :], h_words[:, P * j : P * (j + 1)], ident[:])
+            hT_banks[r] = hT_ps
+
+        def evacuate(r):
+            grouped = work.tile([P, PAIR, PASSES, P, 4], BF16, align_bytes=64)
+            for i in range(PAIR):
+                nc.scalar.copy(out=grouped[:, i].bitcast(F32), in_=zT_banks[r][i][:].rearrange("p g u m -> p g m u"))
+            hT = work.tile([P, PAIR, HALVES, 2 * P], BF16)
+            nc.scalar.copy(out=hT[:].bitcast(F32), in_=hT_banks[r][:])
+            grouped_tiles[r], hT_tiles[r] = grouped, hT
+
+        def quantise(r):
+            codes = work.tile([P, PAIR, PASSES, P], U32, align_bytes=64)
+            planes = work.tile([P, PAIR, PASSES, P], U8, align_bytes=64)
+            nc.vector.quantize_mx(
+                out=codes[:].rearrange("p i g m -> p (i g m)").bitcast(FP8X4),
+                scales=planes[:].rearrange("p i g m -> p (i g m)"),
+                in_=grouped_tiles[r][:].rearrange("p i g m t -> p (i g m t)"),
+            )
+            code_tiles[r], plane_tiles[r] = codes, planes
+
+        def plain(r):
+            plain_banks[r] = []
+            for i in range(PAIR):
+                plain_ps = psum_plain.tile([P, CH], F32)
+                for j in range(HALVES):
+                    for e in range(2):
+                        nc.tensor.matmul(
+                            out=plain_ps[:],
+                            lhsT=hT_tiles[r][:, i, j, e : 2 * P : 2],
+                            rhs=uT[:, j, e, :],
+                            start=(j == 0 and e == 0),
+                            stop=(j == HALVES - 1 and e == 1),
+                        )
+                plain_banks[r].append(plain_ps)
+
+        def mx(r):
+            mx_banks[r] = []
+            for i in range(PAIR):
+                mx_ps = psum_mx.tile([P, CH], F32)
+                for g in range(PASSES):
+                    nc.tensor.matmul_mx(
+                        out=mx_ps[:],
+                        lhsT=code_tiles[r][:, i, g, :].bitcast(FP8X4),
+                        lhsT_scale=plane_tiles[r][:, i, g, :],
+                        rhs=w_words[:, g, :].bitcast(FP4X4),
+                        rhs_scale=w_planes[:, g, :],
+                        start=(g == 0),
+                        stop=(g == PASSES - 1),
+                    )
+                mx_banks[r].append(mx_ps)
+
+        def add_bias(r):
+            pre = work.tile([P, PAIR, CH], F32)
+            for i in range(PAIR):
+                nc.vector.tensor_tensor(out=pre[:, i, :], in0=plain_banks[r][i][:], in1=bias[:], op=ADD)
+            pre_tiles[r] = pre
+
+        def add_mx(r):
+            for i in range(PAIR):
+                nc.vector.tensor_tensor(out=pre_tiles[r][:, i, :], in0=mx_banks[r][i][:], in1=pre_tiles[r][:, i, :], op=ADD)
+
+        def gate(r):
+            gates = work.tile([P, PAIR, CH], F32)
+            nc.scalar.activation(out=gates[:], in_=pre_tiles[r][:], func=SIGMOID)
+            gate_tiles[r] = gates
+
+        def weigh(r):
+            block, first = r // ROUNDS_PER_BLOCK, r % ROUNDS_PER_BLOCK == 0
+            if first:
+                total = totals.tile([P, PAIR, CH], F32)
+                total_tiles[block] = total
+                weighed = total
+            else:
+                total = total_tiles[block]
+                weighed = work.tile([P, PAIR, CH], F32)
+            cells = c_tiles[r][:, :, CH:SIZE]
+            nc.vector.tensor_tensor(out=weighed[:, 0, :], in0=gate_tiles[r][:, 0, :], in1=cells[:, 0, :], op=MULT)
+            nc.gpsimd.tensor_tensor(out=weighed[:, 1, :], in0=gate_tiles[r][:, 1, :], in1=cells[:, 1, :], op=MULT)
+            if not first:
+                nc.gpsimd.tensor_tensor(out=total[:], in0=total[:], in1=weighed[:], op=ADD)
+            if r % ROUNDS_PER_BLOCK == ROUNDS_PER_BLOCK - 1:
+                result = totals.tile([P, CH], F32)
+                nc.vector.tensor_tensor(out=result[:], in0=total[:, 0, :], in1=total[:, 1, :], op=ADD)
+                nc.sync.dma_start(out=out[block * P : (block + 1) * P, :], in_=result[:])
+
+        def run(stage, r):
+            if 0 <= r < ROUNDS:
+                stage(r)
+
+        for s in range(ROUNDS + 3):
+            run(load, s + AHEAD)
+            run(transposes, s)
+            run(evacuate, s)
+            run(add_mx, s - 2)
+            run(weigh, s - 3)
+            run(quantise, s)
+            run(gate, s - 2)
+            run(plain, s - 1)
+            run(add_bias, s - 1)
+            run(mx, s - 1)

@@ -35,7 +35,7 @@ def tile_treelstm_pa_kernel(tc, z_node, z_children, W_f_words, W_f_scales, U_f, 
         work = stack.enter_context(tc.tile_pool(name="work", bufs=3))
         totals = stack.enter_context(tc.tile_pool(name="totals", bufs=2))
         psum_z = stack.enter_context(tc.psum_pool(name="psum_z", bufs=PAIR))
-        psum_h = stack.enter_context(tc.psum_pool(name="psum_h", bufs=1))
+        psum_h = stack.enter_context(tc.psum_pool(name="psum_h", bufs=PAIR))
         psum_plain = stack.enter_context(tc.psum_pool(name="psum_plain", bufs=PAIR))
         psum_mx = stack.enter_context(tc.psum_pool(name="psum_mx", bufs=PAIR))
         stack.enter_context(tc.manual_schedule())
@@ -95,29 +95,42 @@ def tile_treelstm_pa_kernel(tc, z_node, z_children, W_f_words, W_f_scales, U_f, 
         bias = consts.tile([P, CH], F32)
         nc.vector.tensor_copy(out=bias[:], in_=bias_ps[:])
 
-        def transposes(r):
-            zT_banks[r] = []
-            for i in range(PAIR):
-                zT_ps = psum_z.tile([P, PASSES, 2, P], F32)
-                z_words = z_tiles[r][:, i, :].bitcast(F32)
-                for g in range(PASSES):
-                    for u in range(2):
-                        nc.tensor.transpose(zT_ps[:, g, u, :], z_words[:, 2 * P * g + u : 2 * P * (g + 1) : 2], ident[:])
-                zT_banks[r].append(zT_ps)
-            hT_ps = psum_h.tile([P, PAIR, HALVES, P], F32)
-            for i in range(PAIR):
-                h_words = c_tiles[r][:, i, 0:CH].bitcast(F32)
-                for j in range(HALVES):
-                    nc.tensor.transpose(hT_ps[:, i, j, :], h_words[:, P * j : P * (j + 1)], ident[:])
-            hT_banks[r] = hT_ps
+        def live(r):
+            return 0 <= r < ROUNDS
 
-        def evacuate(r):
-            grouped = work.tile([P, PAIR, PASSES, P, 4], BF16, align_bytes=64)
-            for i in range(PAIR):
-                nc.scalar.copy(out=grouped[:, i].bitcast(F32), in_=zT_banks[r][i][:].rearrange("p g u m -> p g m u"))
-            hT = work.tile([P, PAIR, HALVES, 2 * P], BF16)
-            nc.scalar.copy(out=hT[:].bitcast(F32), in_=hT_banks[r][:])
-            grouped_tiles[r], hT_tiles[r] = grouped, hT
+        def plain_and_transposes(s, i):
+            if live(s - 1):
+                plain_ps = psum_plain.tile([P, CH], F32)
+                plain_banks[s - 1, i] = plain_ps
+            if live(s):
+                zT_ps = psum_z.tile([P, PASSES, 2, P], F32)
+                hT_ps = psum_h.tile([P, HALVES, P], F32)
+                zT_banks[s, i], hT_banks[s, i] = zT_ps, hT_ps
+                z_words = z_tiles[s][:, i, :].bitcast(F32)
+                h_words = c_tiles[s][:, i, 0:CH].bitcast(F32)
+            for j in range(HALVES):
+                for e in range(2):
+                    if live(s - 1):
+                        nc.tensor.matmul(
+                            out=plain_ps[:],
+                            lhsT=hT_tiles[s - 1, i][:, j, e : 2 * P : 2],
+                            rhs=uT[:, j, e, :],
+                            start=(j == 0 and e == 0),
+                            stop=(j == HALVES - 1 and e == 1),
+                        )
+                    if live(s):
+                        nc.tensor.transpose(zT_ps[:, j, e, :], z_words[:, 2 * P * j + e : 2 * P * (j + 1) : 2], ident[:])
+                        if e == 0:
+                            nc.tensor.transpose(hT_ps[:, j, :], h_words[:, P * j : P * (j + 1)], ident[:])
+
+        def evacuate(r, i):
+            if i == 0:
+                grouped = work.tile([P, PAIR, PASSES, P, 4], BF16, align_bytes=64)
+                grouped_tiles[r] = grouped
+            nc.scalar.copy(out=grouped_tiles[r][:, i].bitcast(F32), in_=zT_banks[r, i][:].rearrange("p g u m -> p g m u"))
+            hT = work.tile([P, HALVES, 2 * P], BF16, bufs=3 * PAIR)
+            nc.scalar.copy(out=hT[:].bitcast(F32), in_=hT_banks[r, i][:])
+            hT_tiles[r, i] = hT
 
         def quantise(r):
             codes = work.tile([P, PAIR, PASSES, P], U32, align_bytes=64)
@@ -128,21 +141,6 @@ def tile_treelstm_pa_kernel(tc, z_node, z_children, W_f_words, W_f_scales, U_f, 
                 in_=grouped_tiles[r][:].rearrange("p i g m t -> p (i g m t)"),
             )
             code_tiles[r], plane_tiles[r] = codes, planes
-
-        def plain(r):
-            plain_banks[r] = []
-            for i in range(PAIR):
-                plain_ps = psum_plain.tile([P, CH], F32)
-                for j in range(HALVES):
-                    for e in range(2):
-                        nc.tensor.matmul(
-                            out=plain_ps[:],
-                            lhsT=hT_tiles[r][:, i, j, e : 2 * P : 2],
-                            rhs=uT[:, j, e, :],
-                            start=(j == 0 and e == 0),
-                            stop=(j == HALVES - 1 and e == 1),
-                        )
-                plain_banks[r].append(plain_ps)
 
         def mx(r):
             mx_banks[r] = []
@@ -160,11 +158,11 @@ def tile_treelstm_pa_kernel(tc, z_node, z_children, W_f_words, W_f_scales, U_f, 
                     )
                 mx_banks[r].append(mx_ps)
 
-        def add_bias(r):
-            pre = work.tile([P, PAIR, CH], F32)
-            for i in range(PAIR):
-                nc.vector.tensor_tensor(out=pre[:, i, :], in0=plain_banks[r][i][:], in1=bias[:], op=ADD)
-            pre_tiles[r] = pre
+        def add_bias(r, i):
+            if i == 0:
+                pre = work.tile([P, PAIR, CH], F32)
+                pre_tiles[r] = pre
+            nc.vector.tensor_tensor(out=pre_tiles[r][:, i, :], in0=plain_banks[r, i][:], in1=bias[:], op=ADD)
 
         def add_mx(r):
             for i in range(PAIR):
@@ -194,18 +192,18 @@ def tile_treelstm_pa_kernel(tc, z_node, z_children, W_f_words, W_f_scales, U_f, 
                 nc.vector.tensor_tensor(out=result[:], in0=total[:, 0, :], in1=total[:, 1, :], op=ADD)
                 nc.sync.dma_start(out=out[block * P : (block + 1) * P, :], in_=result[:])
 
-        def run(stage, r):
-            if 0 <= r < ROUNDS:
-                stage(r)
+        def run(stage, r, *which):
+            if live(r):
+                stage(r, *which)
 
         for s in range(ROUNDS + 3):
             run(load, s + AHEAD)
-            run(transposes, s)
-            run(evacuate, s)
+            run(quantise, s - 1)
             run(add_mx, s - 2)
             run(weigh, s - 3)
-            run(quantise, s)
+            for i in range(PAIR):
+                plain_and_transposes(s, i)
+                run(evacuate, s, i)
+                run(add_bias, s - 1, i)
             run(gate, s - 2)
-            run(plain, s - 1)
-            run(add_bias, s - 1)
             run(mx, s - 1)

@@ -40,7 +40,7 @@ def tile_treelstm_pa_kernel(tc, z_node, z_children, W_f_words, W_f_scales, U_f, 
         psum_mx = stack.enter_context(tc.psum_pool(name="psum_mx", bufs=PAIR))
         stack.enter_context(tc.manual_schedule())
 
-        z_tiles, c_tiles, zT_banks, hT_banks = {}, {}, {}, {}
+        z_tiles, c_tiles, sorted_tiles, zT_banks, hT_banks = {}, {}, {}, {}, {}
         grouped_tiles, hT_tiles, code_tiles, plane_tiles = {}, {}, {}, {}
         plain_banks, mx_banks, pre_tiles, gate_tiles, total_tiles = {}, {}, {}, {}, {}
 
@@ -98,6 +98,14 @@ def tile_treelstm_pa_kernel(tc, z_node, z_children, W_f_words, W_f_scales, U_f, 
         def live(r):
             return 0 <= r < ROUNDS
 
+        def sort_words(r):
+            z_sorted = work.tile([P, PAIR, PASSES, 2, P], F32)
+            nc.scalar.copy(
+                out=z_sorted[:].rearrange("p i g u m -> p (i g) u m"),
+                in_=z_tiles[r][:].rearrange("p i k -> p (i k)").bitcast(F32).rearrange("p (a m u) -> p a u m", m=P, u=2),
+            )
+            sorted_tiles[r] = z_sorted
+
         def plain_and_transposes(s, i):
             if live(s - 1):
                 plain_ps = psum_plain.tile([P, CH], F32)
@@ -106,22 +114,28 @@ def tile_treelstm_pa_kernel(tc, z_node, z_children, W_f_words, W_f_scales, U_f, 
                 zT_ps = psum_z.tile([P, PASSES, 2, P], F32)
                 hT_ps = psum_h.tile([P, HALVES, P], F32)
                 zT_banks[s, i], hT_banks[s, i] = zT_ps, hT_ps
-                z_words = z_tiles[s][:, i, :].bitcast(F32)
                 h_words = c_tiles[s][:, i, 0:CH].bitcast(F32)
-            for j in range(HALVES):
-                for e in range(2):
-                    if live(s - 1):
-                        nc.tensor.matmul(
-                            out=plain_ps[:],
-                            lhsT=hT_tiles[s - 1, i][:, j, e : 2 * P : 2],
-                            rhs=uT[:, j, e, :],
-                            start=(j == 0 and e == 0),
-                            stop=(j == HALVES - 1 and e == 1),
-                        )
-                    if live(s):
-                        nc.tensor.transpose(zT_ps[:, j, e, :], z_words[:, 2 * P * j + e : 2 * P * (j + 1) : 2], ident[:])
-                        if e == 0:
-                            nc.tensor.transpose(hT_ps[:, j, :], h_words[:, P * j : P * (j + 1)], ident[:])
+
+            def transpose_piece(q):
+                j, u = divmod(q, 3)
+                if u < 2:
+                    nc.tensor.transpose(zT_ps[:, j, u, :], sorted_tiles[s][:, i, j, u, :], ident[:])
+                else:
+                    nc.tensor.transpose(hT_ps[:, j, :], h_words[:, P * j : P * (j + 1)], ident[:])
+
+            for step in range(2 * HALVES):
+                j, e = divmod(step, 2)
+                if live(s - 1):
+                    nc.tensor.matmul(
+                        out=plain_ps[:],
+                        lhsT=hT_tiles[s - 1, i][:, j, e : 2 * P : 2],
+                        rhs=uT[:, j, e, :],
+                        start=(step == 0),
+                        stop=(step == 2 * HALVES - 1),
+                    )
+                if live(s) and step < 2 * HALVES - 1:
+                    transpose_piece(2 * step)
+                    transpose_piece(2 * step + 1)
 
         def evacuate(r, i):
             if i == 0:
@@ -196,6 +210,7 @@ def tile_treelstm_pa_kernel(tc, z_node, z_children, W_f_words, W_f_scales, U_f, 
             if live(r):
                 stage(r, *which)
 
+        sort_words(0)
         for s in range(ROUNDS + 3):
             run(load, s + AHEAD)
             run(quantise, s - 1)
@@ -206,4 +221,5 @@ def tile_treelstm_pa_kernel(tc, z_node, z_children, W_f_words, W_f_scales, U_f, 
                 run(evacuate, s, i)
                 run(add_bias, s - 1, i)
             run(gate, s - 2)
+            run(sort_words, s + 1)
             run(mx, s - 1)

@@ -184,26 +184,31 @@ def tile_treelstm_pa_kernel(tc, z_node, z_children, W_f_words, W_f_scales, U_f, 
 
         def gate(r):
             gates = work.tile([P, PAIR, CH], F32)
-            nc.scalar.activation(out=gates[:], in_=pre_tiles[r][:], func=SIGMOID)
+            for i in range(PAIR):
+                nc.scalar.activation(out=gates[:, i, :], in_=pre_tiles[r][:, i, :], func=SIGMOID)
             gate_tiles[r] = gates
 
         def weigh(r):
-            block, first = r // ROUNDS_PER_BLOCK, r % ROUNDS_PER_BLOCK == 0
-            if first:
+            block, turn = divmod(r, ROUNDS_PER_BLOCK)
+            gates, cells = gate_tiles[r], c_tiles[r][:, :, CH:SIZE]
+            if turn == 0:
                 total = totals.tile([P, PAIR, CH], F32)
                 total_tiles[block] = total
-                weighed = total
+            total = total_tiles[block]
+            if turn < ROUNDS_PER_BLOCK - 1:
+                weighed = total if turn == 0 else work.tile([P, PAIR, CH], F32, name="weighed")
+                nc.vector.tensor_tensor(out=weighed[:, 0, :], in0=gates[:, 0, :], in1=cells[:, 0, :], op=MULT)
+                nc.gpsimd.tensor_tensor(out=weighed[:, 1, :], in0=gates[:, 1, :], in1=cells[:, 1, :], op=MULT)
+                if turn > 0:
+                    nc.gpsimd.tensor_tensor(out=total[:], in0=total[:], in1=weighed[:], op=ADD)
             else:
-                total = total_tiles[block]
-                weighed = work.tile([P, PAIR, CH], F32)
-            cells = c_tiles[r][:, :, CH:SIZE]
-            nc.vector.tensor_tensor(out=weighed[:, 0, :], in0=gate_tiles[r][:, 0, :], in1=cells[:, 0, :], op=MULT)
-            nc.gpsimd.tensor_tensor(out=weighed[:, 1, :], in0=gate_tiles[r][:, 1, :], in1=cells[:, 1, :], op=MULT)
-            if not first:
-                nc.gpsimd.tensor_tensor(out=total[:], in0=total[:], in1=weighed[:], op=ADD)
-            if r % ROUNDS_PER_BLOCK == ROUNDS_PER_BLOCK - 1:
+                last = work.tile([P, PAIR, CH], F32, name="weighed")
+                for i in range(PAIR):
+                    nc.vector.tensor_tensor(out=last[:, i, :], in0=gates[:, i, :], in1=cells[:, i, :], op=MULT)
                 result = totals.tile([P, CH], F32)
-                nc.vector.tensor_tensor(out=result[:], in0=total[:, 0, :], in1=total[:, 1, :], op=ADD)
+                nc.vector.tensor_tensor(out=result[:], in0=last[:, 0, :], in1=last[:, 1, :], op=ADD)
+                for i in range(PAIR):
+                    nc.vector.tensor_tensor(out=result[:], in0=result[:], in1=total[:, i, :], op=ADD)
                 nc.sync.dma_start(out=out[block * P : (block + 1) * P, :], in_=result[:])
 
         def run(stage, r, *which):
@@ -213,13 +218,13 @@ def tile_treelstm_pa_kernel(tc, z_node, z_children, W_f_words, W_f_scales, U_f, 
         sort_words(0)
         for s in range(ROUNDS + 3):
             run(load, s + AHEAD)
+            run(sort_words, s + 1)
             run(quantise, s - 1)
-            run(add_mx, s - 2)
             run(weigh, s - 3)
+            run(add_mx, s - 2)
             for i in range(PAIR):
                 plain_and_transposes(s, i)
                 run(evacuate, s, i)
                 run(add_bias, s - 1, i)
             run(gate, s - 2)
-            run(sort_words, s + 1)
             run(mx, s - 1)

@@ -197,10 +197,10 @@ def tile_treelstm_pa_kernel(tc, z_node, z_children, W_f_words, W_f_scales, U_f, 
             total = total_tiles[block]
             if turn < ROUNDS_PER_BLOCK - 1:
                 weighed = total if turn == 0 else work.tile([P, PAIR, CH], F32, name="weighed")
-                nc.vector.tensor_tensor(out=weighed[:, 0, :], in0=gates[:, 0, :], in1=cells[:, 0, :], op=MULT)
-                nc.gpsimd.tensor_tensor(out=weighed[:, 1, :], in0=gates[:, 1, :], in1=cells[:, 1, :], op=MULT)
-                if turn > 0:
-                    nc.gpsimd.tensor_tensor(out=total[:], in0=total[:], in1=weighed[:], op=ADD)
+                for i, engine in enumerate((nc.vector, nc.gpsimd)):
+                    engine.tensor_tensor(out=weighed[:, i, :], in0=gates[:, i, :], in1=cells[:, i, :], op=MULT)
+                    if turn > 0:
+                        engine.tensor_tensor(out=total[:, i, :], in0=total[:, i, :], in1=weighed[:, i, :], op=ADD)
             else:
                 last = work.tile([P, PAIR, CH], F32, name="weighed")
                 for i in range(PAIR):

@@ -17,7 +17,7 @@ SIGMOID = mybir.ActivationFunctionType.Sigmoid
 P = 128
 NODES, CHILDREN, SIZE, CH = 256, 16, 1024, 512
 PASSES = SIZE // (4 * P)
-HALVES = CH // (2 * P)
+K_TILES = CH // P
 PAIR = 2
 ROUNDS_PER_BLOCK = CHILDREN // PAIR
 ROUNDS = (NODES // P) * ROUNDS_PER_BLOCK
@@ -55,6 +55,8 @@ def tile_treelstm_pa_kernel(tc, z_node, z_children, W_f_words, W_f_scales, U_f, 
 
         ident = consts.tile([P, P], F32)
         make_identity(nc, ident[:])
+        ident_bf = consts.tile([P, P], BF16)
+        make_identity(nc, ident_bf[:])
 
         bias_row = consts.tile([P, CH], BF16)
         nc.vector.memset(bias_row[:], 0.0)
@@ -82,13 +84,12 @@ def tile_treelstm_pa_kernel(tc, z_node, z_children, W_f_words, W_f_scales, U_f, 
         for r in range(1, AHEAD):
             load(r)
 
-        uT = consts.tile([P, HALVES, 2, CH], BF16)
-        for j in range(HALVES):
-            uT_ps = psum_z.tile([P, CH // P, P], F32, tag="zT_ps")
+        uT = consts.tile([P, K_TILES, CH], BF16)
+        for t in range(K_TILES):
+            uT_ps = psum_h.tile([P, CH // P, P], BF16, tag="hT_ps")
             for a in range(CH // P):
-                nc.tensor.transpose(uT_ps[:, a, :], u_sb[:, a, :].bitcast(F32)[:, P * j : P * (j + 1)], ident[:])
-            pairs = uT_ps[:].rearrange("p a c -> p (a c)").bitcast(BF16).rearrange("p (c e) -> p e c", e=2)
-            nc.vector.tensor_copy(out=uT[:, j], in_=pairs)
+                nc.tensor.transpose(uT_ps[:, a, :], u_sb[:, a, P * t : P * (t + 1)], ident_bf[:])
+            nc.vector.tensor_copy(out=uT[:, t, :], in_=uT_ps[:].rearrange("p a c -> p (a c)"))
 
         bias_ps = psum_plain.tile([P, CH], F32, tag="plain_ps")
         nc.tensor.matmul(out=bias_ps[:], lhsT=ones[:], rhs=bias_row[:], start=True, stop=True)
@@ -112,38 +113,40 @@ def tile_treelstm_pa_kernel(tc, z_node, z_children, W_f_words, W_f_scales, U_f, 
                 plain_banks[s - 1, i] = plain_ps
             if live(s):
                 zT_ps = psum_z.tile([P, PASSES, 2, P], F32)
-                hT_ps = psum_h.tile([P, HALVES, P], F32)
+                hT_ps = psum_h.tile([P, K_TILES, P], BF16)
                 zT_banks[s, i], hT_banks[s, i] = zT_ps, hT_ps
-                h_words = c_tiles[s][:, i, 0:CH].bitcast(F32)
 
-            def transpose_piece(q):
-                j, u = divmod(q, 3)
-                if u < 2:
-                    nc.tensor.transpose(zT_ps[:, j, u, :], sorted_tiles[s][:, i, j, u, :], ident[:])
-                else:
-                    nc.tensor.transpose(hT_ps[:, j, :], h_words[:, P * j : P * (j + 1)], ident[:])
+            def transpose_z(q):
+                g, u = divmod(q, 2)
+                nc.tensor.transpose(zT_ps[:, g, u, :], sorted_tiles[s][:, i, g, u, :], ident[:])
 
-            for step in range(2 * HALVES):
-                j, e = divmod(step, 2)
+            def transpose_h(t):
+                nc.tensor.transpose(hT_ps[:, t, :], c_tiles[s][:, i, P * t : P * (t + 1)], ident_bf[:])
+
+            for t in range(K_TILES):
                 if live(s - 1):
                     nc.tensor.matmul(
                         out=plain_ps[:],
-                        lhsT=hT_tiles[s - 1, i][:, j, e : 2 * P : 2],
-                        rhs=uT[:, j, e, :],
-                        start=(step == 0),
-                        stop=(step == 2 * HALVES - 1),
+                        lhsT=hT_tiles[s - 1, i][:, t, :],
+                        rhs=uT[:, t, :],
+                        start=(t == 0),
+                        stop=(t == K_TILES - 1),
                     )
-                if live(s) and step < 2 * HALVES - 1:
-                    transpose_piece(2 * step)
-                    transpose_piece(2 * step + 1)
+                if live(s) and t < 2:
+                    transpose_z(t)
+                    transpose_h(2 * t)
+                    transpose_h(2 * t + 1)
+                if live(s) and t == 2:
+                    transpose_z(2)
+                    transpose_z(3)
 
         def evacuate(r, i):
             if i == 0:
                 grouped = work.tile([P, PAIR, PASSES, P, 4], BF16, align_bytes=64)
                 grouped_tiles[r] = grouped
             nc.scalar.copy(out=grouped_tiles[r][:, i].bitcast(F32), in_=zT_banks[r, i][:].rearrange("p g u m -> p g m u"))
-            hT = work.tile([P, HALVES, 2 * P], BF16, bufs=3 * PAIR)
-            nc.scalar.copy(out=hT[:].bitcast(F32), in_=hT_banks[r, i][:])
+            hT = work.tile([P, K_TILES, P], BF16, bufs=3 * PAIR)
+            nc.scalar.copy(out=hT[:], in_=hT_banks[r, i][:])
             hT_tiles[r, i] = hT
 
         def quantise(r):
@@ -197,10 +200,10 @@ def tile_treelstm_pa_kernel(tc, z_node, z_children, W_f_words, W_f_scales, U_f, 
             total = total_tiles[block]
             if turn < ROUNDS_PER_BLOCK - 1:
                 weighed = total if turn == 0 else work.tile([P, PAIR, CH], F32, name="weighed")
-                for i, engine in enumerate((nc.vector, nc.gpsimd)):
-                    engine.tensor_tensor(out=weighed[:, i, :], in0=gates[:, i, :], in1=cells[:, i, :], op=MULT)
-                    if turn > 0:
-                        engine.tensor_tensor(out=total[:, i, :], in0=total[:, i, :], in1=weighed[:, i, :], op=ADD)
+                nc.vector.tensor_tensor(out=weighed[:, 0, :], in0=gates[:, 0, :], in1=cells[:, 0, :], op=MULT)
+                nc.gpsimd.tensor_tensor(out=weighed[:, 1, :], in0=gates[:, 1, :], in1=cells[:, 1, :], op=MULT)
+                if turn > 0:
+                    nc.gpsimd.tensor_tensor(out=total[:], in0=total[:], in1=weighed[:], op=ADD)
             else:
                 last = work.tile([P, PAIR, CH], F32, name="weighed")
                 for i in range(PAIR):

@@ -200,8 +200,7 @@ def tile_treelstm_pa_kernel(tc, z_node, z_children, W_f_words, W_f_scales, U_f, 
             total = total_tiles[block]
             if turn < ROUNDS_PER_BLOCK - 1:
                 weighed = total if turn == 0 else work.tile([P, PAIR, CH], F32, name="weighed")
-                nc.vector.tensor_tensor(out=weighed[:, 0, :], in0=gates[:, 0, :], in1=cells[:, 0, :], op=MULT)
-                nc.gpsimd.tensor_tensor(out=weighed[:, 1, :], in0=gates[:, 1, :], in1=cells[:, 1, :], op=MULT)
+                nc.vector.tensor_tensor(out=weighed[:], in0=gates[:], in1=cells, op=MULT)
                 if turn > 0:
                     nc.gpsimd.tensor_tensor(out=total[:], in0=total[:], in1=weighed[:], op=ADD)
             else:

@@ -48,11 +48,16 @@ def tile_treelstm_pa_kernel(tc, z_node, z_children, W_f_words, W_f_scales, U_f, 
             nodes = slice((r // ROUNDS_PER_BLOCK) * P, (r // ROUNDS_PER_BLOCK + 1) * P)
             children = slice((r % ROUNDS_PER_BLOCK) * PAIR, (r % ROUNDS_PER_BLOCK + 1) * PAIR)
             z_sb = z_pool.tile([P, PAIR, SIZE], BF16)
-            nc.sync.dma_start(out=z_sb[:], in_=z_node[nodes, children, :])
+            if r == 0:
+                for i in range(PAIR):
+                    nc.sync.dma_start(out=z_sb[:, i, :], in_=z_node[nodes, i, :])
+            else:
+                nc.sync.dma_start(out=z_sb[:], in_=z_node[nodes, children, :])
             c_sb = c_pool.tile([P, PAIR, SIZE], BF16)
             nc.sync.dma_start(out=c_sb[:], in_=z_children[nodes, children, :])
             z_tiles[r], c_tiles[r] = z_sb, c_sb
 
+        load(0)
         ident = consts.tile([P, P], F32)
         make_identity(nc, ident[:])
         ident_bf = consts.tile([P, P], BF16)
@@ -60,7 +65,6 @@ def tile_treelstm_pa_kernel(tc, z_node, z_children, W_f_words, W_f_scales, U_f, 
 
         bias_row = consts.tile([P, CH], BF16)
         nc.vector.memset(bias_row[:], 0.0)
-        nc.sync.dma_start(out=bias_row[0:1, :], in_=b_f.rearrange("(o n) -> o n", o=1))
 
         warm = consts.tile([P, 1], F32)
         nc.vector.memset(warm[:], 0.0)
@@ -71,9 +75,10 @@ def tile_treelstm_pa_kernel(tc, z_node, z_children, W_f_words, W_f_scales, U_f, 
         ones = consts.tile([P, P], BF16)
         nc.vector.memset(ones[:], 1.0)
 
+        nc.sync.dma_start(out=bias_row[0:1, :], in_=b_f.rearrange("(o n) -> o n", o=1))
         u_sb = consts.tile([P, CH // P, CH], BF16)
         nc.sync.dma_start(out=u_sb[:], in_=U_f.rearrange("(a p) k -> p a k", p=P))
-        load(0)
+        load(1)
         w_words = consts.tile([P, PASSES, 2 * CH], U8, align_bytes=64)
         nc.sync.dma_start(out=w_words[:].bitcast(I32), in_=W_f_words.bitcast(I32).rearrange("g p n -> p g n"))
         for quadrant in range(4):
@@ -81,30 +86,35 @@ def tile_treelstm_pa_kernel(tc, z_node, z_children, W_f_words, W_f_scales, U_f, 
                 out=w_planes[32 * quadrant : 32 * quadrant + 4].bitcast(I32),
                 in_=W_f_scales.bitcast(I32)[:, 4 * quadrant : 4 * quadrant + 4, :].rearrange("g q n -> q g n"),
             )
-        for r in range(1, AHEAD):
+        for r in range(2, AHEAD):
             load(r)
 
         uT = consts.tile([P, K_TILES, CH], BF16)
-        for t in range(K_TILES):
-            uT_ps = psum_h.tile([P, CH // P, P], BF16, tag="hT_ps")
-            for a in range(CH // P):
-                nc.tensor.transpose(uT_ps[:, a, :], u_sb[:, a, P * t : P * (t + 1)], ident_bf[:])
-            nc.vector.tensor_copy(out=uT[:, t, :], in_=uT_ps[:].rearrange("p a c -> p (a c)"))
-
-        bias_ps = psum_plain.tile([P, CH], F32, tag="plain_ps")
-        nc.tensor.matmul(out=bias_ps[:], lhsT=ones[:], rhs=bias_row[:], start=True, stop=True)
         bias = consts.tile([P, CH], F32)
-        nc.vector.tensor_copy(out=bias[:], in_=bias_ps[:])
+
+        def prepare_plain_operands():
+            for t in range(K_TILES):
+                if t % 2 == 0:
+                    uT_ps = psum_mx.tile([P, CH // P, P], BF16, tag="mx_ps")
+                else:
+                    uT_ps = psum_plain.tile([P, CH // P, P], BF16, tag="plain_ps")
+                for a in range(CH // P):
+                    nc.tensor.transpose(uT_ps[:, a, :], u_sb[:, a, P * t : P * (t + 1)], ident_bf[:])
+                nc.vector.tensor_copy(out=uT[:, t, :], in_=uT_ps[:].rearrange("p a c -> p (a c)"))
+            bias_ps = psum_mx.tile([P, CH], F32, tag="mx_ps")
+            nc.tensor.matmul(out=bias_ps[:], lhsT=ones[:], rhs=bias_row[:], start=True, stop=True)
+            nc.vector.tensor_copy(out=bias[:], in_=bias_ps[:])
 
         def live(r):
             return 0 <= r < ROUNDS
 
         def sort_words(r):
             z_sorted = work.tile([P, PAIR, PASSES, 2, P], F32)
-            nc.scalar.copy(
-                out=z_sorted[:].rearrange("p i g u m -> p (i g) u m"),
-                in_=z_tiles[r][:].rearrange("p i k -> p (i k)").bitcast(F32).rearrange("p (a m u) -> p a u m", m=P, u=2),
-            )
+            for part in [slice(i, i + 1) for i in range(PAIR)] if r == 0 else [slice(0, PAIR)]:
+                nc.scalar.copy(
+                    out=z_sorted[:, part].rearrange("p i g u m -> p (i g) u m"),
+                    in_=z_tiles[r][:, part, :].rearrange("p i k -> p (i k)").bitcast(F32).rearrange("p (a m u) -> p a u m", m=P, u=2),
+                )
             sorted_tiles[r] = z_sorted
 
         def plain_and_transposes(s, i):
@@ -198,19 +208,24 @@ def tile_treelstm_pa_kernel(tc, z_node, z_children, W_f_words, W_f_scales, U_f, 
                 total = totals.tile([P, PAIR, CH], F32)
                 total_tiles[block] = total
             total = total_tiles[block]
-            if turn < ROUNDS_PER_BLOCK - 1:
+            if r < ROUNDS - 1:
                 weighed = total if turn == 0 else work.tile([P, PAIR, CH], F32, name="weighed")
                 nc.vector.tensor_tensor(out=weighed[:], in0=gates[:], in1=cells, op=MULT)
                 if turn > 0:
                     nc.gpsimd.tensor_tensor(out=total[:], in0=total[:], in1=weighed[:], op=ADD)
+                elif block > 0:
+                    before = total_tiles[block - 1]
+                    result = totals.tile([P, CH], F32)
+                    nc.vector.tensor_tensor(out=result[:], in0=before[:, 0, :], in1=before[:, 1, :], op=ADD)
+                    nc.sync.dma_start(out=out[(block - 1) * P : block * P, :], in_=result[:])
             else:
                 last = work.tile([P, PAIR, CH], F32, name="weighed")
                 for i in range(PAIR):
                     nc.vector.tensor_tensor(out=last[:, i, :], in0=gates[:, i, :], in1=cells[:, i, :], op=MULT)
+                for i in range(PAIR):
+                    nc.vector.tensor_tensor(out=last[:, i, :], in0=last[:, i, :], in1=total[:, i, :], op=ADD)
                 result = totals.tile([P, CH], F32)
                 nc.vector.tensor_tensor(out=result[:], in0=last[:, 0, :], in1=last[:, 1, :], op=ADD)
-                for i in range(PAIR):
-                    nc.vector.tensor_tensor(out=result[:], in0=result[:], in1=total[:, i, :], op=ADD)
                 nc.sync.dma_start(out=out[block * P : (block + 1) * P, :], in_=result[:])
 
         def run(stage, r, *which):
@@ -220,13 +235,22 @@ def tile_treelstm_pa_kernel(tc, z_node, z_children, W_f_words, W_f_scales, U_f, 
         sort_words(0)
         for s in range(ROUNDS + 3):
             run(load, s + AHEAD)
-            run(sort_words, s + 1)
+            if s == 1:
+                prepare_plain_operands()
+            if s > 0:
+                run(sort_words, s + 1)
             run(quantise, s - 1)
-            run(weigh, s - 3)
-            run(add_mx, s - 2)
+            if live(s - 1):
+                run(weigh, s - 3)
+                run(add_mx, s - 2)
+            else:
+                run(add_mx, s - 2)
+                run(weigh, s - 3)
             for i in range(PAIR):
                 plain_and_transposes(s, i)
                 run(evacuate, s, i)
                 run(add_bias, s - 1, i)
+            if s == 0:
+                sort_words(1)
             run(gate, s - 2)
             run(mx, s - 1)

@@ -22,6 +22,7 @@ PAIR = 2
 ROUNDS_PER_BLOCK = CHILDREN // PAIR
 ROUNDS = (NODES // P) * ROUNDS_PER_BLOCK
 AHEAD = 3
+IN_PIECES = 2
 
 FLOPS = 2 * NODES * CHILDREN * CH * (SIZE + CH)
 
@@ -42,20 +43,26 @@ def tile_treelstm_pa_kernel(tc, z_node, z_children, W_f_words, W_f_scales, U_f, 
 
         z_tiles, c_tiles, sorted_tiles, zT_banks, hT_banks = {}, {}, {}, {}, {}
         grouped_tiles, hT_tiles, code_tiles, plane_tiles = {}, {}, {}, {}
-        plain_banks, mx_banks, pre_tiles, gate_tiles, total_tiles = {}, {}, {}, {}, {}
+        plain_banks, mx_banks, pre_tiles, gate_tiles, total_tiles, weighed_tiles = {}, {}, {}, {}, {}, {}
 
         def load(r):
             nodes = slice((r // ROUNDS_PER_BLOCK) * P, (r // ROUNDS_PER_BLOCK + 1) * P)
             children = slice((r % ROUNDS_PER_BLOCK) * PAIR, (r % ROUNDS_PER_BLOCK + 1) * PAIR)
             z_sb = z_pool.tile([P, PAIR, SIZE], BF16)
-            if r == 0:
+            c_sb = c_pool.tile([P, PAIR, SIZE], BF16)
+            if r < IN_PIECES:
                 for i in range(PAIR):
-                    nc.sync.dma_start(out=z_sb[:, i, :], in_=z_node[nodes, i, :])
+                    nc.sync.dma_start(out=z_sb[:, i, :], in_=z_node[nodes, children.start + i, :])
+                nc.sync.dma_start(out=c_sb[:, :, 0:CH], in_=z_children[nodes, children, 0:CH])
             else:
                 nc.sync.dma_start(out=z_sb[:], in_=z_node[nodes, children, :])
-            c_sb = c_pool.tile([P, PAIR, SIZE], BF16)
-            nc.sync.dma_start(out=c_sb[:], in_=z_children[nodes, children, :])
+                nc.sync.dma_start(out=c_sb[:], in_=z_children[nodes, children, :])
             z_tiles[r], c_tiles[r] = z_sb, c_sb
+
+        def load_cells(r):
+            nodes = slice((r // ROUNDS_PER_BLOCK) * P, (r // ROUNDS_PER_BLOCK + 1) * P)
+            children = slice((r % ROUNDS_PER_BLOCK) * PAIR, (r % ROUNDS_PER_BLOCK + 1) * PAIR)
+            nc.sync.dma_start(out=c_tiles[r][:, :, CH:SIZE], in_=z_children[nodes, children, CH:SIZE])
 
         load(0)
         ident = consts.tile([P, P], F32)
@@ -88,6 +95,8 @@ def tile_treelstm_pa_kernel(tc, z_node, z_children, W_f_words, W_f_scales, U_f, 
             )
         for r in range(2, AHEAD):
             load(r)
+        for r in range(IN_PIECES):
+            load_cells(r)
 
         uT = consts.tile([P, K_TILES, CH], BF16)
         bias = consts.tile([P, CH], F32)
@@ -110,28 +119,42 @@ def tile_treelstm_pa_kernel(tc, z_node, z_children, W_f_words, W_f_scales, U_f, 
 
         def sort_words(r):
             z_sorted = work.tile([P, PAIR, PASSES, 2, P], F32)
-            for part in [slice(i, i + 1) for i in range(PAIR)] if r == 0 else [slice(0, PAIR)]:
+            for part in [slice(i, i + 1) for i in range(PAIR)] if r < IN_PIECES else [slice(0, PAIR)]:
                 nc.scalar.copy(
                     out=z_sorted[:, part].rearrange("p i g u m -> p (i g) u m"),
                     in_=z_tiles[r][:, part, :].rearrange("p i k -> p (i k)").bitcast(F32).rearrange("p (a m u) -> p a u m", m=P, u=2),
                 )
             sorted_tiles[r] = z_sorted
 
+        def open_banks(r, i):
+            zT_ps = psum_z.tile([P, PASSES, 2, P], F32)
+            hT_ps = psum_h.tile([P, K_TILES, P], BF16)
+            zT_banks[r, i], hT_banks[r, i] = zT_ps, hT_ps
+
+        def transpose_z(r, i, q):
+            g, u = divmod(q, 2)
+            nc.tensor.transpose(zT_banks[r, i][:, g, u, :], sorted_tiles[r][:, i, g, u, :], ident[:])
+
+        def transpose_h(r, i, t):
+            nc.tensor.transpose(hT_banks[r, i][:, t, :], c_tiles[r][:, i, P * t : P * (t + 1)], ident_bf[:])
+
+        def first_transposes():
+            for i in range(PAIR):
+                open_banks(0, i)
+                for q in range(2 * PASSES):
+                    transpose_z(0, i, q)
+                evacuate_z(0, i)
+            for i in range(PAIR):
+                for t in range(K_TILES):
+                    transpose_h(0, i, t)
+                evacuate_h(0, i)
+
         def plain_and_transposes(s, i):
             if live(s - 1):
                 plain_ps = psum_plain.tile([P, CH], F32)
                 plain_banks[s - 1, i] = plain_ps
             if live(s):
-                zT_ps = psum_z.tile([P, PASSES, 2, P], F32)
-                hT_ps = psum_h.tile([P, K_TILES, P], BF16)
-                zT_banks[s, i], hT_banks[s, i] = zT_ps, hT_ps
-
-            def transpose_z(q):
-                g, u = divmod(q, 2)
-                nc.tensor.transpose(zT_ps[:, g, u, :], sorted_tiles[s][:, i, g, u, :], ident[:])
-
-            def transpose_h(t):
-                nc.tensor.transpose(hT_ps[:, t, :], c_tiles[s][:, i, P * t : P * (t + 1)], ident_bf[:])
+                open_banks(s, i)
 
             for t in range(K_TILES):
                 if live(s - 1):
@@ -143,18 +166,20 @@ def tile_treelstm_pa_kernel(tc, z_node, z_children, W_f_words, W_f_scales, U_f, 
                         stop=(t == K_TILES - 1),
                     )
                 if live(s) and t < 2:
-                    transpose_z(t)
-                    transpose_h(2 * t)
-                    transpose_h(2 * t + 1)
+                    transpose_z(s, i, t)
+                    transpose_h(s, i, 2 * t)
+                    transpose_h(s, i, 2 * t + 1)
                 if live(s) and t == 2:
-                    transpose_z(2)
-                    transpose_z(3)
+                    transpose_z(s, i, 2)
+                    transpose_z(s, i, 3)
 
-        def evacuate(r, i):
+        def evacuate_z(r, i):
             if i == 0:
                 grouped = work.tile([P, PAIR, PASSES, P, 4], BF16, align_bytes=64)
                 grouped_tiles[r] = grouped
             nc.scalar.copy(out=grouped_tiles[r][:, i].bitcast(F32), in_=zT_banks[r, i][:].rearrange("p g u m -> p g m u"))
+
+        def evacuate_h(r, i):
             hT = work.tile([P, K_TILES, P], BF16, bufs=3 * PAIR)
             nc.scalar.copy(out=hT[:], in_=hT_banks[r, i][:])
             hT_tiles[r, i] = hT
@@ -211,8 +236,10 @@ def tile_treelstm_pa_kernel(tc, z_node, z_children, W_f_words, W_f_scales, U_f, 
             if r < ROUNDS - 1:
                 weighed = total if turn == 0 else work.tile([P, PAIR, CH], F32, name="weighed")
                 nc.vector.tensor_tensor(out=weighed[:], in0=gates[:], in1=cells, op=MULT)
-                if turn > 0:
+                if 0 < turn and r < ROUNDS - 2:
                     nc.gpsimd.tensor_tensor(out=total[:], in0=total[:], in1=weighed[:], op=ADD)
+                elif r == ROUNDS - 2:
+                    weighed_tiles[r] = weighed
                 elif block > 0:
                     before = total_tiles[block - 1]
                     result = totals.tile([P, CH], F32)
@@ -220,10 +247,12 @@ def tile_treelstm_pa_kernel(tc, z_node, z_children, W_f_words, W_f_scales, U_f, 
                     nc.sync.dma_start(out=out[(block - 1) * P : block * P, :], in_=result[:])
             else:
                 last = work.tile([P, PAIR, CH], F32, name="weighed")
+                previous = weighed_tiles[r - 1]
+                nc.vector.tensor_tensor(out=last[:, 0, :], in0=gates[:, 0, :], in1=cells[:, 0, :], op=MULT)
+                nc.vector.tensor_tensor(out=previous[:], in0=previous[:], in1=total[:], op=ADD)
+                nc.vector.tensor_tensor(out=last[:, 1, :], in0=gates[:, 1, :], in1=cells[:, 1, :], op=MULT)
                 for i in range(PAIR):
-                    nc.vector.tensor_tensor(out=last[:, i, :], in0=gates[:, i, :], in1=cells[:, i, :], op=MULT)
-                for i in range(PAIR):
-                    nc.vector.tensor_tensor(out=last[:, i, :], in0=last[:, i, :], in1=total[:, i, :], op=ADD)
+                    nc.vector.tensor_tensor(out=last[:, i, :], in0=last[:, i, :], in1=previous[:, i, :], op=ADD)
                 result = totals.tile([P, CH], F32)
                 nc.vector.tensor_tensor(out=result[:], in0=last[:, 0, :], in1=last[:, 1, :], op=ADD)
                 nc.sync.dma_start(out=out[block * P : (block + 1) * P, :], in_=result[:])
@@ -237,7 +266,7 @@ def tile_treelstm_pa_kernel(tc, z_node, z_children, W_f_words, W_f_scales, U_f, 
             run(load, s + AHEAD)
             if s == 1:
                 prepare_plain_operands()
-            if s > 0:
+            if s >= IN_PIECES:
                 run(sort_words, s + 1)
             run(quantise, s - 1)
             if live(s - 1):
@@ -246,11 +275,16 @@ def tile_treelstm_pa_kernel(tc, z_node, z_children, W_f_words, W_f_scales, U_f, 
             else:
                 run(add_mx, s - 2)
                 run(weigh, s - 3)
-            for i in range(PAIR):
-                plain_and_transposes(s, i)
-                run(evacuate, s, i)
-                run(add_bias, s - 1, i)
             if s == 0:
+                first_transposes()
                 sort_words(1)
+            else:
+                for i in range(PAIR):
+                    plain_and_transposes(s, i)
+                    run(evacuate_z, s, i)
+                    run(evacuate_h, s, i)
+                    run(add_bias, s - 1, i)
+                    if s == 1 and i == 0:
+                        sort_words(2)
             run(gate, s - 2)
             run(mx, s - 1)

@@ -67,8 +67,6 @@ def tile_treelstm_pa_kernel(tc, z_node, z_children, W_f_words, W_f_scales, U_f, 
         load(0)
         ident = consts.tile([P, P], F32)
         make_identity(nc, ident[:])
-        ident_bf = consts.tile([P, P], BF16)
-        make_identity(nc, ident_bf[:])
 
         bias_row = consts.tile([P, CH], BF16)
         nc.vector.memset(bias_row[:], 0.0)
@@ -98,18 +96,21 @@ def tile_treelstm_pa_kernel(tc, z_node, z_children, W_f_words, W_f_scales, U_f, 
         for r in range(IN_PIECES):
             load_cells(r)
 
-        uT = consts.tile([P, K_TILES, CH], BF16)
+        uT = consts.tile([P, 2, 2, CH], BF16)
         bias = consts.tile([P, CH], F32)
 
         def prepare_plain_operands():
-            for t in range(K_TILES):
-                if t % 2 == 0:
-                    uT_ps = psum_mx.tile([P, CH // P, P], BF16, tag="mx_ps")
+            for u in range(2):
+                if u == 0:
+                    uT_ps = psum_mx.tile([P, CH // P, P], F32, tag="mx_ps")
                 else:
-                    uT_ps = psum_plain.tile([P, CH // P, P], BF16, tag="plain_ps")
+                    uT_ps = psum_plain.tile([P, CH // P, P], F32, tag="plain_ps")
                 for a in range(CH // P):
-                    nc.tensor.transpose(uT_ps[:, a, :], u_sb[:, a, P * t : P * (t + 1)], ident_bf[:])
-                nc.vector.tensor_copy(out=uT[:, t, :], in_=uT_ps[:].rearrange("p a c -> p (a c)"))
+                    nc.tensor.transpose(uT_ps[:, a, :], u_sb[:, a, :].bitcast(F32)[:, P * u : P * (u + 1)], ident[:])
+                nc.vector.tensor_copy(
+                    out=uT[:, u, :, :],
+                    in_=uT_ps[:].rearrange("p a c -> p (a c)").bitcast(BF16).rearrange("p (c e) -> p e c", e=2),
+                )
             bias_ps = psum_mx.tile([P, CH], F32, tag="mx_ps")
             nc.tensor.matmul(out=bias_ps[:], lhsT=ones[:], rhs=bias_row[:], start=True, stop=True)
             nc.vector.tensor_copy(out=bias[:], in_=bias_ps[:])
@@ -128,15 +129,15 @@ def tile_treelstm_pa_kernel(tc, z_node, z_children, W_f_words, W_f_scales, U_f, 
 
         def open_banks(r, i):
             zT_ps = psum_z.tile([P, PASSES, 2, P], F32)
-            hT_ps = psum_h.tile([P, K_TILES, P], BF16)
+            hT_ps = psum_h.tile([P, 2, P], F32)
             zT_banks[r, i], hT_banks[r, i] = zT_ps, hT_ps
 
         def transpose_z(r, i, q):
             g, u = divmod(q, 2)
             nc.tensor.transpose(zT_banks[r, i][:, g, u, :], sorted_tiles[r][:, i, g, u, :], ident[:])
 
-        def transpose_h(r, i, t):
-            nc.tensor.transpose(hT_banks[r, i][:, t, :], c_tiles[r][:, i, P * t : P * (t + 1)], ident_bf[:])
+        def transpose_h(r, i, u):
+            nc.tensor.transpose(hT_banks[r, i][:, u, :], c_tiles[r][:, i, 0:CH].bitcast(F32)[:, P * u : P * (u + 1)], ident[:])
 
         def first_transposes():
             for i in range(PAIR):
@@ -145,8 +146,8 @@ def tile_treelstm_pa_kernel(tc, z_node, z_children, W_f_words, W_f_scales, U_f, 
                     transpose_z(0, i, q)
                 evacuate_z(0, i)
             for i in range(PAIR):
-                for t in range(K_TILES):
-                    transpose_h(0, i, t)
+                for u in range(2):
+                    transpose_h(0, i, u)
                 evacuate_h(0, i)
 
         def plain_and_transposes(s, i):
@@ -160,15 +161,14 @@ def tile_treelstm_pa_kernel(tc, z_node, z_children, W_f_words, W_f_scales, U_f, 
                 if live(s - 1):
                     nc.tensor.matmul(
                         out=plain_ps[:],
-                        lhsT=hT_tiles[s - 1, i][:, t, :],
-                        rhs=uT[:, t, :],
+                        lhsT=hT_tiles[s - 1, i][:, t // 2, t % 2, :],
+                        rhs=uT[:, t // 2, t % 2, :],
                         start=(t == 0),
                         stop=(t == K_TILES - 1),
                     )
                 if live(s) and t < 2:
                     transpose_z(s, i, t)
-                    transpose_h(s, i, 2 * t)
-                    transpose_h(s, i, 2 * t + 1)
+                    transpose_h(s, i, t)
                 if live(s) and t == 2:
                     transpose_z(s, i, 2)
                     transpose_z(s, i, 3)
@@ -180,8 +180,12 @@ def tile_treelstm_pa_kernel(tc, z_node, z_children, W_f_words, W_f_scales, U_f, 
             nc.scalar.copy(out=grouped_tiles[r][:, i].bitcast(F32), in_=zT_banks[r, i][:].rearrange("p g u m -> p g m u"))
 
         def evacuate_h(r, i):
-            hT = work.tile([P, K_TILES, P], BF16, bufs=3 * PAIR)
-            nc.scalar.copy(out=hT[:], in_=hT_banks[r, i][:])
+            hT = work.tile([P, 2, 2, P], BF16, bufs=3 * PAIR)
+            halves = hT_banks[r, i][:].rearrange("p u m -> p (u m)").bitcast(BF16).rearrange("p (u m e) -> p u e m", u=2, e=2)
+            if i == 0:
+                nc.scalar.copy(out=hT[:], in_=halves)
+            else:
+                nc.vector.tensor_copy(out=hT[:], in_=halves)
             hT_tiles[r, i] = hT
 
         def quantise(r):
@@ -282,9 +286,11 @@ def tile_treelstm_pa_kernel(tc, z_node, z_children, W_f_words, W_f_scales, U_f, 
                 for i in range(PAIR):
                     plain_and_transposes(s, i)
                     run(evacuate_z, s, i)
-                    run(evacuate_h, s, i)
+                    if i == 0:
+                        run(evacuate_h, s, i)
                     run(add_bias, s - 1, i)
                     if s == 1 and i == 0:
                         sort_words(2)
+                run(evacuate_h, s, 1)
             run(gate, s - 2)
             run(mx, s - 1)

@@ -41,7 +41,7 @@ def tile_treelstm_pa_kernel(tc, z_node, z_children, W_f_words, W_f_scales, U_f, 
         psum_mx = stack.enter_context(tc.psum_pool(name="psum_mx", bufs=PAIR))
         stack.enter_context(tc.manual_schedule())
 
-        z_tiles, c_tiles, sorted_tiles, zT_banks, hT_banks = {}, {}, {}, {}, {}
+        z_tiles, c_tiles, zT_banks, hT_banks = {}, {}, {}, {}
         grouped_tiles, hT_tiles, code_tiles, plane_tiles = {}, {}, {}, {}
         plain_banks, mx_banks, pre_tiles, gate_tiles, total_tiles, weighed_tiles = {}, {}, {}, {}, {}, {}
 
@@ -93,8 +93,6 @@ def tile_treelstm_pa_kernel(tc, z_node, z_children, W_f_words, W_f_scales, U_f, 
             )
         for r in range(2, AHEAD):
             load(r)
-        for r in range(IN_PIECES):
-            load_cells(r)
 
         uT = consts.tile([P, 2, 2, CH], BF16)
         bias = consts.tile([P, CH], F32)
@@ -118,15 +116,6 @@ def tile_treelstm_pa_kernel(tc, z_node, z_children, W_f_words, W_f_scales, U_f, 
         def live(r):
             return 0 <= r < ROUNDS
 
-        def sort_words(r):
-            z_sorted = work.tile([P, PAIR, PASSES, 2, P], F32)
-            for part in [slice(i, i + 1) for i in range(PAIR)] if r < IN_PIECES else [slice(0, PAIR)]:
-                nc.scalar.copy(
-                    out=z_sorted[:, part].rearrange("p i g u m -> p (i g) u m"),
-                    in_=z_tiles[r][:, part, :].rearrange("p i k -> p (i k)").bitcast(F32).rearrange("p (a m u) -> p a u m", m=P, u=2),
-                )
-            sorted_tiles[r] = z_sorted
-
         def open_banks(r, i):
             zT_ps = psum_z.tile([P, PASSES, 2, P], F32)
             hT_ps = psum_h.tile([P, 2, P], F32)
@@ -134,7 +123,8 @@ def tile_treelstm_pa_kernel(tc, z_node, z_children, W_f_words, W_f_scales, U_f, 
 
         def transpose_z(r, i, q):
             g, u = divmod(q, 2)
-            nc.tensor.transpose(zT_banks[r, i][:, g, u, :], sorted_tiles[r][:, i, g, u, :], ident[:])
+            words = z_tiles[r][:, i, :].bitcast(F32)
+            nc.tensor.transpose(zT_banks[r, i][:, g, u, :], words[:, 2 * P * g + u : 2 * P * (g + 1) : 2], ident[:])
 
         def transpose_h(r, i, u):
             nc.tensor.transpose(hT_banks[r, i][:, u, :], c_tiles[r][:, i, 0:CH].bitcast(F32)[:, P * u : P * (u + 1)], ident[:])
@@ -166,12 +156,13 @@ def tile_treelstm_pa_kernel(tc, z_node, z_children, W_f_words, W_f_scales, U_f, 
                         start=(t == 0),
                         stop=(t == K_TILES - 1),
                     )
-                if live(s) and t < 2:
-                    transpose_z(s, i, t)
-                    transpose_h(s, i, t)
-                if live(s) and t == 2:
-                    transpose_z(s, i, 2)
-                    transpose_z(s, i, 3)
+                if live(s):
+                    if t < K_TILES - 1 or i == 0:
+                        transpose_z(s, i, t)
+                    if t < 2:
+                        transpose_h(s, i, t)
+                    if t == K_TILES - 2 and i == 1:
+                        transpose_z(s, i, t + 1)
 
         def evacuate_z(r, i):
             if i == 0:
@@ -182,10 +173,7 @@ def tile_treelstm_pa_kernel(tc, z_node, z_children, W_f_words, W_f_scales, U_f, 
         def evacuate_h(r, i):
             hT = work.tile([P, 2, 2, P], BF16, bufs=3 * PAIR)
             halves = hT_banks[r, i][:].rearrange("p u m -> p (u m)").bitcast(BF16).rearrange("p (u m e) -> p u e m", u=2, e=2)
-            if i == 0:
-                nc.scalar.copy(out=hT[:], in_=halves)
-            else:
-                nc.vector.tensor_copy(out=hT[:], in_=halves)
+            nc.scalar.copy(out=hT[:], in_=halves)
             hT_tiles[r, i] = hT
 
         def quantise(r):
@@ -265,13 +253,10 @@ def tile_treelstm_pa_kernel(tc, z_node, z_children, W_f_words, W_f_scales, U_f, 
             if live(r):
                 stage(r, *which)
 
-        sort_words(0)
         for s in range(ROUNDS + 3):
             run(load, s + AHEAD)
             if s == 1:
                 prepare_plain_operands()
-            if s >= IN_PIECES:
-                run(sort_words, s + 1)
             run(quantise, s - 1)
             if live(s - 1):
                 run(weigh, s - 3)
@@ -281,16 +266,13 @@ def tile_treelstm_pa_kernel(tc, z_node, z_children, W_f_words, W_f_scales, U_f, 
                 run(weigh, s - 3)
             if s == 0:
                 first_transposes()
-                sort_words(1)
             else:
                 for i in range(PAIR):
                     plain_and_transposes(s, i)
                     run(evacuate_z, s, i)
-                    if i == 0:
-                        run(evacuate_h, s, i)
+                    run(evacuate_h, s, i)
                     run(add_bias, s - 1, i)
-                    if s == 1 and i == 0:
-                        sort_words(2)
-                run(evacuate_h, s, 1)
+            if s < IN_PIECES:
+                load_cells(s)
             run(gate, s - 2)
             run(mx, s - 1)

@@ -23,6 +23,7 @@ ROUNDS_PER_BLOCK = CHILDREN // PAIR
 ROUNDS = (NODES // P) * ROUNDS_PER_BLOCK
 AHEAD = 3
 IN_PIECES = 2
+GPSIMD_COLUMNS = 768
 
 FLOPS = 2 * NODES * CHILDREN * CH * (SIZE + CH)
 
@@ -44,6 +45,7 @@ def tile_treelstm_pa_kernel(tc, z_node, z_children, W_f_words, W_f_scales, U_f, 
         z_tiles, c_tiles, zT_banks, hT_banks = {}, {}, {}, {}
         grouped_tiles, hT_tiles, code_tiles, plane_tiles = {}, {}, {}, {}
         plain_banks, mx_banks, pre_tiles, gate_tiles, total_tiles, weighed_tiles = {}, {}, {}, {}, {}, {}
+        shared_sums = {}
 
         def load(r):
             nodes = slice((r // ROUNDS_PER_BLOCK) * P, (r // ROUNDS_PER_BLOCK + 1) * P)
@@ -225,11 +227,21 @@ def tile_treelstm_pa_kernel(tc, z_node, z_children, W_f_words, W_f_scales, U_f, 
                 total = totals.tile([P, PAIR, CH], F32)
                 total_tiles[block] = total
             total = total_tiles[block]
+            if r - 1 in shared_sums:
+                sum_before, products_before = shared_sums[r - 1]
+                nc.vector.tensor_tensor(
+                    out=sum_before[:, GPSIMD_COLUMNS:], in0=sum_before[:, GPSIMD_COLUMNS:], in1=products_before[:, GPSIMD_COLUMNS:], op=ADD
+                )
             if r < ROUNDS - 1:
                 weighed = total if turn == 0 else work.tile([P, PAIR, CH], F32, name="weighed")
                 nc.vector.tensor_tensor(out=weighed[:], in0=gates[:], in1=cells, op=MULT)
                 if 0 < turn and r < ROUNDS - 2:
-                    nc.gpsimd.tensor_tensor(out=total[:], in0=total[:], in1=weighed[:], op=ADD)
+                    flat_total = total[:].rearrange("p i c -> p (i c)")
+                    flat_weighed = weighed[:].rearrange("p i c -> p (i c)")
+                    nc.gpsimd.tensor_tensor(
+                        out=flat_total[:, :GPSIMD_COLUMNS], in0=flat_total[:, :GPSIMD_COLUMNS], in1=flat_weighed[:, :GPSIMD_COLUMNS], op=ADD
+                    )
+                    shared_sums[r] = (flat_total, flat_weighed)
                 elif r == ROUNDS - 2:
                     weighed_tiles[r] = weighed
                 elif block > 0:

@@ -25,6 +25,8 @@ AHEAD = 3
 IN_PIECES = 2
 GPSIMD_COLUMNS = 768
 
+TENSOR_BIAS_ROUNDS = 2
+
 FLOPS = 2 * NODES * CHILDREN * CH * (SIZE + CH)
 
 
@@ -47,26 +49,37 @@ def tile_treelstm_pa_kernel(tc, z_node, z_children, W_f_words, W_f_scales, U_f, 
         plain_banks, mx_banks, pre_tiles, gate_tiles, total_tiles, weighed_tiles = {}, {}, {}, {}, {}, {}
         shared_sums = {}
 
+        def load_hidden(r):
+            nodes = slice((r // ROUNDS_PER_BLOCK) * P, (r // ROUNDS_PER_BLOCK + 1) * P)
+            children = slice((r % ROUNDS_PER_BLOCK) * PAIR, (r % ROUNDS_PER_BLOCK + 1) * PAIR)
+            c_sb = c_pool.tile([P, PAIR, SIZE], BF16)
+            nc.sync.dma_start(out=c_sb[:, :, 0:CH], in_=z_children[nodes, children, 0:CH])
+            c_tiles[r] = c_sb
+
         def load(r):
             nodes = slice((r // ROUNDS_PER_BLOCK) * P, (r // ROUNDS_PER_BLOCK + 1) * P)
             children = slice((r % ROUNDS_PER_BLOCK) * PAIR, (r % ROUNDS_PER_BLOCK + 1) * PAIR)
             z_sb = z_pool.tile([P, PAIR, SIZE], BF16)
-            c_sb = c_pool.tile([P, PAIR, SIZE], BF16)
             if r < IN_PIECES:
                 for i in range(PAIR):
                     nc.sync.dma_start(out=z_sb[:, i, :], in_=z_node[nodes, children.start + i, :])
-                nc.sync.dma_start(out=c_sb[:, :, 0:CH], in_=z_children[nodes, children, 0:CH])
+                    if r > 0 and i == 0:
+                        load_hidden(r)
             else:
+                c_sb = c_pool.tile([P, PAIR, SIZE], BF16)
                 nc.sync.dma_start(out=z_sb[:], in_=z_node[nodes, children, :])
                 nc.sync.dma_start(out=c_sb[:], in_=z_children[nodes, children, :])
-            z_tiles[r], c_tiles[r] = z_sb, c_sb
+                c_tiles[r] = c_sb
+            z_tiles[r] = z_sb
 
         def load_cells(r):
             nodes = slice((r // ROUNDS_PER_BLOCK) * P, (r // ROUNDS_PER_BLOCK + 1) * P)
             children = slice((r % ROUNDS_PER_BLOCK) * PAIR, (r % ROUNDS_PER_BLOCK + 1) * PAIR)
             nc.sync.dma_start(out=c_tiles[r][:, :, CH:SIZE], in_=z_children[nodes, children, CH:SIZE])
 
-        load(0)
+        load_hidden(0)
+        u_sb = consts.tile([P, CH // P, CH], BF16)
+        nc.sync.dma_start(out=u_sb[:], in_=U_f.rearrange("(a p) k -> p a k", p=P))
         ident = consts.tile([P, P], F32)
         make_identity(nc, ident[:])
 
@@ -83,8 +96,7 @@ def tile_treelstm_pa_kernel(tc, z_node, z_children, W_f_words, W_f_scales, U_f, 
         nc.vector.memset(ones[:], 1.0)
 
         nc.sync.dma_start(out=bias_row[0:1, :], in_=b_f.rearrange("(o n) -> o n", o=1))
-        u_sb = consts.tile([P, CH // P, CH], BF16)
-        nc.sync.dma_start(out=u_sb[:], in_=U_f.rearrange("(a p) k -> p a k", p=P))
+        load(0)
         load(1)
         w_words = consts.tile([P, PASSES, 2 * CH], U8, align_bytes=64)
         nc.sync.dma_start(out=w_words[:].bitcast(I32), in_=W_f_words.bitcast(I32).rearrange("g p n -> p g n"))
@@ -99,6 +111,11 @@ def tile_treelstm_pa_kernel(tc, z_node, z_children, W_f_words, W_f_scales, U_f, 
         uT = consts.tile([P, 2, 2, CH], BF16)
         bias = consts.tile([P, CH], F32)
 
+        def spread_bias():
+            bias_ps = psum_mx.tile([P, CH], F32, tag="mx_ps")
+            nc.tensor.matmul(out=bias_ps[:], lhsT=ones[:], rhs=bias_row[:], start=True, stop=True)
+            nc.vector.tensor_copy(out=bias[:], in_=bias_ps[:])
+
         def prepare_plain_operands():
             for u in range(2):
                 if u == 0:
@@ -107,16 +124,17 @@ def tile_treelstm_pa_kernel(tc, z_node, z_children, W_f_words, W_f_scales, U_f, 
                     uT_ps = psum_plain.tile([P, CH // P, P], F32, tag="plain_ps")
                 for a in range(CH // P):
                     nc.tensor.transpose(uT_ps[:, a, :], u_sb[:, a, :].bitcast(F32)[:, P * u : P * (u + 1)], ident[:])
-                nc.vector.tensor_copy(
-                    out=uT[:, u, :, :],
-                    in_=uT_ps[:].rearrange("p a c -> p (a c)").bitcast(BF16).rearrange("p (c e) -> p e c", e=2),
-                )
-            bias_ps = psum_mx.tile([P, CH], F32, tag="mx_ps")
-            nc.tensor.matmul(out=bias_ps[:], lhsT=ones[:], rhs=bias_row[:], start=True, stop=True)
-            nc.vector.tensor_copy(out=bias[:], in_=bias_ps[:])
+                halves = uT_ps[:].rearrange("p a c -> p (a c)").bitcast(BF16).rearrange("p (c e) -> p e c", e=2)
+                if u == 0:
+                    nc.vector.tensor_copy(out=uT[:, u, :, :], in_=halves)
+                else:
+                    nc.scalar.copy(out=uT[:, u, :, :], in_=halves)
 
         def live(r):
             return 0 <= r < ROUNDS
+
+        def biased_by_tensor(r):
+            return r >= ROUNDS - TENSOR_BIAS_ROUNDS
 
         def open_banks(r, i):
             zT_ps = psum_z.tile([P, PASSES, 2, P], F32)
@@ -134,13 +152,15 @@ def tile_treelstm_pa_kernel(tc, z_node, z_children, W_f_words, W_f_scales, U_f, 
         def first_transposes():
             for i in range(PAIR):
                 open_banks(0, i)
-                for q in range(2 * PASSES):
-                    transpose_z(0, i, q)
-                evacuate_z(0, i)
-            for i in range(PAIR):
                 for u in range(2):
                     transpose_h(0, i, u)
                 evacuate_h(0, i)
+            prepare_plain_operands()
+            spread_bias()
+            for i in range(PAIR):
+                for q in range(2 * PASSES):
+                    transpose_z(0, i, q)
+                evacuate_z(0, i)
 
         def plain_and_transposes(s, i):
             if live(s - 1):
@@ -149,13 +169,16 @@ def tile_treelstm_pa_kernel(tc, z_node, z_children, W_f_words, W_f_scales, U_f, 
             if live(s):
                 open_banks(s, i)
 
+            bias_first = live(s - 1) and biased_by_tensor(s - 1)
+            if bias_first:
+                nc.tensor.matmul(out=plain_ps[:], lhsT=ones[:], rhs=bias_row[:], start=True, stop=False)
             for t in range(K_TILES):
                 if live(s - 1):
                     nc.tensor.matmul(
                         out=plain_ps[:],
                         lhsT=hT_tiles[s - 1, i][:, t // 2, t % 2, :],
                         rhs=uT[:, t // 2, t % 2, :],
-                        start=(t == 0),
+                        start=(t == 0 and not bias_first),
                         stop=(t == K_TILES - 1),
                     )
                 if live(s):
@@ -168,9 +191,13 @@ def tile_treelstm_pa_kernel(tc, z_node, z_children, W_f_words, W_f_scales, U_f, 
 
         def evacuate_z(r, i):
             if i == 0:
-                grouped = work.tile([P, PAIR, PASSES, P, 4], BF16, align_bytes=64)
-                grouped_tiles[r] = grouped
-            nc.scalar.copy(out=grouped_tiles[r][:, i].bitcast(F32), in_=zT_banks[r, i][:].rearrange("p g u m -> p g m u"))
+                pair_grouped = work.tile([P, PAIR, PASSES, P, 4], BF16, align_bytes=64, name="pair_grouped")
+                grouped_tiles[r] = pair_grouped
+            grouped, words = grouped_tiles[r][:, i].bitcast(F32), zT_banks[r, i][:].rearrange("p g u m -> p g m u")
+            if (r, i) == (0, 0):
+                nc.vector.tensor_copy(out=grouped, in_=words)
+            else:
+                nc.scalar.copy(out=grouped, in_=words)
 
         def evacuate_h(r, i):
             hT = work.tile([P, 2, 2, P], BF16, bufs=3 * PAIR)
@@ -208,7 +235,10 @@ def tile_treelstm_pa_kernel(tc, z_node, z_children, W_f_words, W_f_scales, U_f, 
             if i == 0:
                 pre = work.tile([P, PAIR, CH], F32)
                 pre_tiles[r] = pre
-            nc.vector.tensor_tensor(out=pre_tiles[r][:, i, :], in0=plain_banks[r, i][:], in1=bias[:], op=ADD)
+            if biased_by_tensor(r):
+                nc.scalar.copy(out=pre_tiles[r][:, i, :], in_=plain_banks[r, i][:])
+            else:
+                nc.vector.tensor_tensor(out=pre_tiles[r][:, i, :], in0=plain_banks[r, i][:], in1=bias[:], op=ADD)
 
         def add_mx(r):
             for i in range(PAIR):
@@ -267,10 +297,8 @@ def tile_treelstm_pa_kernel(tc, z_node, z_children, W_f_words, W_f_scales, U_f, 
 
         for s in range(ROUNDS + 3):
             run(load, s + AHEAD)
-            if s == 1:
-                prepare_plain_operands()
             run(quantise, s - 1)
-            if live(s - 1):
+            if live(s) and (s - 3) % ROUNDS_PER_BLOCK > 0:
                 run(weigh, s - 3)
                 run(add_mx, s - 2)
             else:

@@ -25,7 +25,11 @@ AHEAD = 3
 IN_PIECES = 2
 GPSIMD_COLUMNS = 768
 
-TENSOR_BIAS_ROUNDS = 2
+def biased_by_tensor(r, i):
+    return r >= ROUNDS - 2 and i == 0
+
+
+SUMMED_AT_END = ROUNDS - 3
 
 FLOPS = 2 * NODES * CHILDREN * CH * (SIZE + CH)
 
@@ -133,9 +137,6 @@ def tile_treelstm_pa_kernel(tc, z_node, z_children, W_f_words, W_f_scales, U_f, 
         def live(r):
             return 0 <= r < ROUNDS
 
-        def biased_by_tensor(r):
-            return r >= ROUNDS - TENSOR_BIAS_ROUNDS
-
         def open_banks(r, i):
             zT_ps = psum_z.tile([P, PASSES, 2, P], F32)
             hT_ps = psum_h.tile([P, 2, P], F32)
@@ -169,7 +170,7 @@ def tile_treelstm_pa_kernel(tc, z_node, z_children, W_f_words, W_f_scales, U_f, 
             if live(s):
                 open_banks(s, i)
 
-            bias_first = live(s - 1) and biased_by_tensor(s - 1)
+            bias_first = live(s - 1) and biased_by_tensor(s - 1, i)
             if bias_first:
                 nc.tensor.matmul(out=plain_ps[:], lhsT=ones[:], rhs=bias_row[:], start=True, stop=False)
             for t in range(K_TILES):
@@ -235,7 +236,7 @@ def tile_treelstm_pa_kernel(tc, z_node, z_children, W_f_words, W_f_scales, U_f, 
             if i == 0:
                 pre = work.tile([P, PAIR, CH], F32)
                 pre_tiles[r] = pre
-            if biased_by_tensor(r):
+            if biased_by_tensor(r, i):
                 nc.scalar.copy(out=pre_tiles[r][:, i, :], in_=plain_banks[r, i][:])
             else:
                 nc.vector.tensor_tensor(out=pre_tiles[r][:, i, :], in0=plain_banks[r, i][:], in1=bias[:], op=ADD)
@@ -244,11 +245,18 @@ def tile_treelstm_pa_kernel(tc, z_node, z_children, W_f_words, W_f_scales, U_f, 
             for i in range(PAIR):
                 nc.vector.tensor_tensor(out=pre_tiles[r][:, i, :], in0=mx_banks[r][i][:], in1=pre_tiles[r][:, i, :], op=ADD)
 
-        def gate(r):
-            gates = work.tile([P, PAIR, CH], F32)
-            for i in range(PAIR):
-                nc.scalar.activation(out=gates[:, i, :], in_=pre_tiles[r][:, i, :], func=SIGMOID)
-            gate_tiles[r] = gates
+        def gate(r, i):
+            if i == 0:
+                gates = work.tile([P, PAIR, CH], F32)
+                gate_tiles[r] = gates
+            nc.scalar.activation(out=gate_tiles[r][:, i, :], in_=pre_tiles[r][:, i, :], func=SIGMOID)
+
+        def add_share(r):
+            if r in shared_sums:
+                sum_before, products_before = shared_sums[r]
+                nc.vector.tensor_tensor(
+                    out=sum_before[:, GPSIMD_COLUMNS:], in0=sum_before[:, GPSIMD_COLUMNS:], in1=products_before[:, GPSIMD_COLUMNS:], op=ADD
+                )
 
         def weigh(r):
             block, turn = divmod(r, ROUNDS_PER_BLOCK)
@@ -257,51 +265,68 @@ def tile_treelstm_pa_kernel(tc, z_node, z_children, W_f_words, W_f_scales, U_f, 
                 total = totals.tile([P, PAIR, CH], F32)
                 total_tiles[block] = total
             total = total_tiles[block]
-            if r - 1 in shared_sums:
-                sum_before, products_before = shared_sums[r - 1]
-                nc.vector.tensor_tensor(
-                    out=sum_before[:, GPSIMD_COLUMNS:], in0=sum_before[:, GPSIMD_COLUMNS:], in1=products_before[:, GPSIMD_COLUMNS:], op=ADD
+            weighed = total if turn == 0 else work.tile([P, PAIR, CH], F32, name="weighed")
+            nc.vector.tensor_tensor(out=weighed[:], in0=gates[:], in1=cells, op=MULT)
+            weighed_tiles[r] = weighed
+            if 0 < turn and r < SUMMED_AT_END:
+                flat_total = total[:].rearrange("p i c -> p (i c)")
+                flat_weighed = weighed[:].rearrange("p i c -> p (i c)")
+                nc.gpsimd.tensor_tensor(
+                    out=flat_total[:, :GPSIMD_COLUMNS], in0=flat_total[:, :GPSIMD_COLUMNS], in1=flat_weighed[:, :GPSIMD_COLUMNS], op=ADD
                 )
-            if r < ROUNDS - 1:
-                weighed = total if turn == 0 else work.tile([P, PAIR, CH], F32, name="weighed")
-                nc.vector.tensor_tensor(out=weighed[:], in0=gates[:], in1=cells, op=MULT)
-                if 0 < turn and r < ROUNDS - 2:
-                    flat_total = total[:].rearrange("p i c -> p (i c)")
-                    flat_weighed = weighed[:].rearrange("p i c -> p (i c)")
-                    nc.gpsimd.tensor_tensor(
-                        out=flat_total[:, :GPSIMD_COLUMNS], in0=flat_total[:, :GPSIMD_COLUMNS], in1=flat_weighed[:, :GPSIMD_COLUMNS], op=ADD
-                    )
-                    shared_sums[r] = (flat_total, flat_weighed)
-                elif r == ROUNDS - 2:
-                    weighed_tiles[r] = weighed
-                elif block > 0:
-                    before = total_tiles[block - 1]
-                    result = totals.tile([P, CH], F32)
-                    nc.vector.tensor_tensor(out=result[:], in0=before[:, 0, :], in1=before[:, 1, :], op=ADD)
-                    nc.sync.dma_start(out=out[(block - 1) * P : block * P, :], in_=result[:])
-            else:
-                last = work.tile([P, PAIR, CH], F32, name="weighed")
-                previous = weighed_tiles[r - 1]
-                nc.vector.tensor_tensor(out=last[:, 0, :], in0=gates[:, 0, :], in1=cells[:, 0, :], op=MULT)
-                nc.vector.tensor_tensor(out=previous[:], in0=previous[:], in1=total[:], op=ADD)
-                nc.vector.tensor_tensor(out=last[:, 1, :], in0=gates[:, 1, :], in1=cells[:, 1, :], op=MULT)
-                for i in range(PAIR):
-                    nc.vector.tensor_tensor(out=last[:, i, :], in0=last[:, i, :], in1=previous[:, i, :], op=ADD)
-                result = totals.tile([P, CH], F32)
-                nc.vector.tensor_tensor(out=result[:], in0=last[:, 0, :], in1=last[:, 1, :], op=ADD)
-                nc.sync.dma_start(out=out[block * P : (block + 1) * P, :], in_=result[:])
+                shared_sums[r] = (flat_total, flat_weighed)
+
+        def fold_total(block):
+            total = total_tiles[block]
+            folded = totals.tile([P, CH], F32)
+            nc.gpsimd.tensor_tensor(out=folded[:], in0=total[:, 0, :], in1=total[:, 1, :], op=ADD)
+            return folded
+
+        def weigh_shared(r):
+            weighed = work.tile([P, PAIR, CH], F32, name="weighed")
+            for i, engine in enumerate((nc.gpsimd, nc.vector)):
+                engine.tensor_tensor(out=weighed[:, i, :], in0=gate_tiles[r][:, i, :], in1=c_tiles[r][:, i, CH:SIZE], op=MULT)
+            weighed_tiles[r] = weighed
+
+        def sum_on_tensor(tiles):
+            sum_ps = psum_plain.tile([P, CH], F32, tag="plain_ps")
+            for k, tile in enumerate(tiles):
+                nc.tensor.matmul(out=sum_ps[:], lhsT=ident[:], rhs=tile, start=(k == 0), stop=(k == len(tiles) - 1))
+            return sum_ps
+
+        def finish(folded, sum_ps):
+            r = ROUNDS - 1
+            last = work.tile([P, PAIR, CH], F32, name="weighed")
+            before = weighed_tiles[r - 1]
+            for i in range(PAIR):
+                nc.vector.tensor_tensor(out=last[:, i, :], in0=gate_tiles[r][:, i, :], in1=c_tiles[r][:, i, CH:SIZE], op=MULT)
+            nc.vector.tensor_tensor(out=last[:, 0, :], in0=last[:, 0, :], in1=folded[:], op=ADD)
+            nc.vector.tensor_tensor(out=last[:, 1, :], in0=last[:, 1, :], in1=before[:, 1, :], op=ADD)
+            result = totals.tile([P, CH], F32)
+            halves = [slice(0, CH // 2), slice(CH // 2, CH)]
+            for half in halves:
+                nc.vector.tensor_tensor(out=last[:, 0, half], in0=last[:, 0, half], in1=last[:, 1, half], op=ADD)
+            for half in halves:
+                nc.vector.tensor_tensor(out=result[:, half], in0=sum_ps[:, half], in1=last[:, 0, half], op=ADD)
+                nc.sync.dma_start(out=out[NODES - P : NODES, half], in_=result[:, half])
 
         def run(stage, r, *which):
             if live(r):
                 stage(r, *which)
 
-        for s in range(ROUNDS + 3):
+        for s in range(ROUNDS + 1):
             run(load, s + AHEAD)
             run(quantise, s - 1)
+            add_share(s - 4)
             if live(s) and (s - 3) % ROUNDS_PER_BLOCK > 0:
                 run(weigh, s - 3)
                 run(add_mx, s - 2)
             else:
+                if live(s - 4):
+                    block = (s - 4) // ROUNDS_PER_BLOCK
+                    folded = fold_total(block)
+                    if live(s):
+                        nc.sync.dma_start(out=out[block * P : (block + 1) * P, :], in_=folded[:])
                 run(add_mx, s - 2)
                 run(weigh, s - 3)
             if s == 0:
@@ -310,9 +335,17 @@ def tile_treelstm_pa_kernel(tc, z_node, z_children, W_f_words, W_f_scales, U_f, 
                 for i in range(PAIR):
                     plain_and_transposes(s, i)
                     run(evacuate_z, s, i)
-                    run(evacuate_h, s, i)
+                    if i == 1:
+                        for child in range(PAIR):
+                            run(gate, s - 2, child)
                     run(add_bias, s - 1, i)
+                    run(evacuate_h, s, i)
             if s < IN_PIECES:
                 load_cells(s)
-            run(gate, s - 2)
             run(mx, s - 1)
+        add_mx(ROUNDS - 1)
+        for child in range(PAIR):
+            gate(ROUNDS - 1, child)
+        weigh_shared(ROUNDS - 2)
+        sum_ps = sum_on_tensor([weighed_tiles[SUMMED_AT_END][:, 0, :], weighed_tiles[SUMMED_AT_END][:, 1, :], weighed_tiles[ROUNDS - 2][:, 0, :]])
+        finish(folded, sum_ps)

@@ -81,6 +81,18 @@ def tile_treelstm_pa_kernel(tc, z_node, z_children, W_f_words, W_f_scales, U_f, 
             children = slice((r % ROUNDS_PER_BLOCK) * PAIR, (r % ROUNDS_PER_BLOCK + 1) * PAIR)
             nc.sync.dma_start(out=c_tiles[r][:, :, CH:SIZE], in_=z_children[nodes, children, CH:SIZE])
 
+        ones = consts.tile([P, P], BF16)
+        nc.vector.memset(ones[:], 1.0)
+        idle_columns = consts.tile([P, CH], BF16)
+        nc.vector.memset(idle_columns[:], 0.0)
+        idle_ps = psum_plain.tile([P, CH], F32, tag="plain_ps")
+
+        def keep_clock(count):
+            for k in range(count):
+                nc.tensor.matmul(out=idle_ps[:], lhsT=ones[:], rhs=idle_columns[:], start=True, stop=True)
+
+        keep_clock(4)
+
         load_hidden(0)
         u_sb = consts.tile([P, CH // P, CH], BF16)
         nc.sync.dma_start(out=u_sb[:], in_=U_f.rearrange("(a p) k -> p a k", p=P))
@@ -96,8 +108,6 @@ def tile_treelstm_pa_kernel(tc, z_node, z_children, W_f_words, W_f_scales, U_f, 
 
         w_planes = consts.tile([P, PASSES, CH], U8, align_bytes=64)
         nc.vector.memset(w_planes[:].bitcast(I32), 0)
-        ones = consts.tile([P, P], BF16)
-        nc.vector.memset(ones[:], 1.0)
 
         nc.sync.dma_start(out=bias_row[0:1, :], in_=b_f.rearrange("(o n) -> o n", o=1))
         load(0)
@@ -156,12 +166,15 @@ def tile_treelstm_pa_kernel(tc, z_node, z_children, W_f_words, W_f_scales, U_f, 
                 for u in range(2):
                     transpose_h(0, i, u)
                 evacuate_h(0, i)
+            keep_clock(2)
             prepare_plain_operands()
-            spread_bias()
+            keep_clock(1)
             for i in range(PAIR):
                 for q in range(2 * PASSES):
                     transpose_z(0, i, q)
                 evacuate_z(0, i)
+                if i == 0:
+                    spread_bias()
 
         def plain_and_transposes(s, i):
             if live(s - 1):

@@ -23,7 +23,7 @@ ROUNDS_PER_BLOCK = CHILDREN // PAIR
 ROUNDS = (NODES // P) * ROUNDS_PER_BLOCK
 AHEAD = 3
 IN_PIECES = 2
-GPSIMD_COLUMNS = 768
+GPSIMD_COLUMNS = 832
 
 def biased_by_tensor(r, i):
     return r >= ROUNDS - 2 and i == 0
@@ -91,11 +91,12 @@ def tile_treelstm_pa_kernel(tc, z_node, z_children, W_f_words, W_f_scales, U_f, 
             for k in range(count):
                 nc.tensor.matmul(out=idle_ps[:], lhsT=ones[:], rhs=idle_columns[:], start=True, stop=True)
 
-        keep_clock(4)
+        keep_clock(3)
 
         load_hidden(0)
         u_sb = consts.tile([P, CH // P, CH], BF16)
-        nc.sync.dma_start(out=u_sb[:], in_=U_f.rearrange("(a p) k -> p a k", p=P))
+        for half in range(2):
+            nc.sync.dma_start(out=u_sb[:, 2 * half : 2 * half + 2, :], in_=U_f.rearrange("(a p) k -> p a k", p=P)[:, 2 * half : 2 * half + 2, :])
         ident = consts.tile([P, P], F32)
         make_identity(nc, ident[:])
 
@@ -131,18 +132,20 @@ def tile_treelstm_pa_kernel(tc, z_node, z_children, W_f_words, W_f_scales, U_f, 
             nc.vector.tensor_copy(out=bias[:], in_=bias_ps[:])
 
         def prepare_plain_operands():
-            for u in range(2):
-                if u == 0:
-                    uT_ps = psum_mx.tile([P, CH // P, P], F32, tag="mx_ps")
+            for half in range(2):
+                if half == 0:
+                    uT_ps = psum_mx.tile([P, 2, 2, P], F32, tag="mx_ps")
                 else:
-                    uT_ps = psum_plain.tile([P, CH // P, P], F32, tag="plain_ps")
-                for a in range(CH // P):
-                    nc.tensor.transpose(uT_ps[:, a, :], u_sb[:, a, :].bitcast(F32)[:, P * u : P * (u + 1)], ident[:])
-                halves = uT_ps[:].rearrange("p a c -> p (a c)").bitcast(BF16).rearrange("p (c e) -> p e c", e=2)
-                if u == 0:
-                    nc.vector.tensor_copy(out=uT[:, u, :, :], in_=halves)
+                    uT_ps = psum_plain.tile([P, 2, 2, P], F32, tag="plain_ps")
+                for a in range(2):
+                    for u in range(2):
+                        nc.tensor.transpose(uT_ps[:, u, a, :], u_sb[:, 2 * half + a, :].bitcast(F32)[:, P * u : P * (u + 1)], ident[:])
+                columns = slice(half * CH // 2, (half + 1) * CH // 2)
+                halves = uT_ps[:].rearrange("p u a c -> p (u a c)").bitcast(BF16).rearrange("p (u c e) -> p u e c", u=2, e=2)
+                if half == 0:
+                    nc.vector.tensor_copy(out=uT[:, :, :, columns], in_=halves)
                 else:
-                    nc.scalar.copy(out=uT[:, u, :, :], in_=halves)
+                    nc.scalar.copy(out=uT[:, :, :, columns], in_=halves)
 
         def live(r):
             return 0 <= r < ROUNDS
@@ -166,7 +169,7 @@ def tile_treelstm_pa_kernel(tc, z_node, z_children, W_f_words, W_f_scales, U_f, 
                 for u in range(2):
                     transpose_h(0, i, u)
                 evacuate_h(0, i)
-            keep_clock(2)
+            keep_clock(1)
             prepare_plain_operands()
             keep_clock(1)
             for i in range(PAIR):

@@ -23,8 +23,6 @@ ROUNDS_PER_BLOCK = CHILDREN // PAIR
 ROUNDS = (NODES // P) * ROUNDS_PER_BLOCK
 AHEAD = 3
 IN_PIECES = 2
-GPSIMD_COLUMNS = 832
-
 def biased_by_tensor(r, i):
     return r >= ROUNDS - 2 and i == 0
 
@@ -51,7 +49,6 @@ def tile_treelstm_pa_kernel(tc, z_node, z_children, W_f_words, W_f_scales, U_f, 
         z_tiles, c_tiles, zT_banks, hT_banks = {}, {}, {}, {}
         grouped_tiles, hT_tiles, code_tiles, plane_tiles = {}, {}, {}, {}
         plain_banks, mx_banks, pre_tiles, gate_tiles, total_tiles, weighed_tiles = {}, {}, {}, {}, {}, {}
-        shared_sums = {}
 
         def load_hidden(r):
             nodes = slice((r // ROUNDS_PER_BLOCK) * P, (r // ROUNDS_PER_BLOCK + 1) * P)
@@ -267,30 +264,27 @@ def tile_treelstm_pa_kernel(tc, z_node, z_children, W_f_words, W_f_scales, U_f, 
                 gate_tiles[r] = gates
             nc.scalar.activation(out=gate_tiles[r][:, i, :], in_=pre_tiles[r][:, i, :], func=SIGMOID)
 
-        def add_share(r):
-            if r in shared_sums:
-                sum_before, products_before = shared_sums[r]
-                nc.vector.tensor_tensor(
-                    out=sum_before[:, GPSIMD_COLUMNS:], in0=sum_before[:, GPSIMD_COLUMNS:], in1=products_before[:, GPSIMD_COLUMNS:], op=ADD
-                )
+        def products(r, engine, out):
+            engine.tensor_tensor(out=out[:], in0=gate_tiles[r][:], in1=c_tiles[r][:, :, CH:SIZE], op=MULT)
+            weighed_tiles[r] = out
 
         def weigh(r):
+            weighed = work.tile([P, PAIR, CH], F32, name="shared_weighed", bufs=1)
+            products(r, nc.gpsimd, weighed)
+
+        def weigh_at_end(r):
+            weighed = work.tile([P, PAIR, CH], F32, name="weighed")
+            products(r, nc.vector, weighed)
+
+        def add_up(r):
             block, turn = divmod(r, ROUNDS_PER_BLOCK)
-            gates, cells = gate_tiles[r], c_tiles[r][:, :, CH:SIZE]
             if turn == 0:
                 total = totals.tile([P, PAIR, CH], F32)
                 total_tiles[block] = total
-            total = total_tiles[block]
-            weighed = total if turn == 0 else work.tile([P, PAIR, CH], F32, name="weighed")
-            nc.vector.tensor_tensor(out=weighed[:], in0=gates[:], in1=cells, op=MULT)
-            weighed_tiles[r] = weighed
-            if 0 < turn and r < SUMMED_AT_END:
-                flat_total = total[:].rearrange("p i c -> p (i c)")
-                flat_weighed = weighed[:].rearrange("p i c -> p (i c)")
-                nc.gpsimd.tensor_tensor(
-                    out=flat_total[:, :GPSIMD_COLUMNS], in0=flat_total[:, :GPSIMD_COLUMNS], in1=flat_weighed[:, :GPSIMD_COLUMNS], op=ADD
-                )
-                shared_sums[r] = (flat_total, flat_weighed)
+                products(r, nc.vector, total)
+            else:
+                total = total_tiles[block]
+                nc.vector.tensor_tensor(out=total[:], in0=total[:], in1=weighed_tiles[r][:], op=ADD)
 
         def fold_total(block):
             total = total_tiles[block]
@@ -333,29 +327,29 @@ def tile_treelstm_pa_kernel(tc, z_node, z_children, W_f_words, W_f_scales, U_f, 
         for s in range(ROUNDS + 1):
             run(load, s + AHEAD)
             run(quantise, s - 1)
-            add_share(s - 4)
-            if live(s) and (s - 3) % ROUNDS_PER_BLOCK > 0:
-                run(weigh, s - 3)
-                run(add_mx, s - 2)
-            else:
-                if live(s - 4):
-                    block = (s - 4) // ROUNDS_PER_BLOCK
+            if live(s - 3):
+                block, turn = divmod(s - 3, ROUNDS_PER_BLOCK)
+                if turn == 0 and block > 0:
+                    nc.sync.dma_start(out=out[(block - 1) * P : block * P, :], in_=fold_total(block - 1)[:])
+                elif s - 3 == SUMMED_AT_END:
                     folded = fold_total(block)
-                    if live(s):
-                        nc.sync.dma_start(out=out[block * P : (block + 1) * P, :], in_=folded[:])
-                run(add_mx, s - 2)
-                run(weigh, s - 3)
+                elif turn > 0:
+                    weigh(s - 3)
+            run(add_mx, s - 2)
+            if s - 3 == SUMMED_AT_END:
+                weigh_at_end(s - 3)
             if s == 0:
                 first_transposes()
             else:
                 for i in range(PAIR):
                     plain_and_transposes(s, i)
                     run(evacuate_z, s, i)
-                    if i == 1:
-                        for child in range(PAIR):
-                            run(gate, s - 2, child)
                     run(add_bias, s - 1, i)
                     run(evacuate_h, s, i)
+            for child in range(PAIR):
+                run(gate, s - 2, child)
+            if s - 3 < SUMMED_AT_END:
+                run(add_up, s - 3)
             if s < IN_PIECES:
                 load_cells(s)
             run(mx, s - 1)

@@ -23,6 +23,8 @@ ROUNDS_PER_BLOCK = CHILDREN // PAIR
 ROUNDS = (NODES // P) * ROUNDS_PER_BLOCK
 AHEAD = 3
 IN_PIECES = 2
+GPSIMD_COLUMNS = 480
+
 def biased_by_tensor(r, i):
     return r >= ROUNDS - 2 and i == 0
 
@@ -264,13 +266,15 @@ def tile_treelstm_pa_kernel(tc, z_node, z_children, W_f_words, W_f_scales, U_f, 
                 gate_tiles[r] = gates
             nc.scalar.activation(out=gate_tiles[r][:, i, :], in_=pre_tiles[r][:, i, :], func=SIGMOID)
 
-        def products(r, engine, out):
-            engine.tensor_tensor(out=out[:], in0=gate_tiles[r][:], in1=c_tiles[r][:, :, CH:SIZE], op=MULT)
+        def products(r, engine, out, columns=slice(0, CH)):
+            cells = slice(CH + columns.start, CH + columns.stop)
+            engine.tensor_tensor(out=out[:, :, columns], in0=gate_tiles[r][:, :, columns], in1=c_tiles[r][:, :, cells], op=MULT)
             weighed_tiles[r] = out
 
         def weigh(r):
             weighed = work.tile([P, PAIR, CH], F32, name="shared_weighed", bufs=1)
-            products(r, nc.gpsimd, weighed)
+            products(r, nc.gpsimd, weighed, slice(0, GPSIMD_COLUMNS))
+            products(r, nc.vector, weighed, slice(GPSIMD_COLUMNS, CH))
 
         def weigh_at_end(r):
             weighed = work.tile([P, PAIR, CH], F32, name="weighed")
@@ -307,15 +311,13 @@ def tile_treelstm_pa_kernel(tc, z_node, z_children, W_f_words, W_f_scales, U_f, 
         def finish(folded, sum_ps):
             r = ROUNDS - 1
             last = work.tile([P, PAIR, CH], F32, name="weighed")
-            before = weighed_tiles[r - 1]
             for i in range(PAIR):
                 nc.vector.tensor_tensor(out=last[:, i, :], in0=gate_tiles[r][:, i, :], in1=c_tiles[r][:, i, CH:SIZE], op=MULT)
-            nc.vector.tensor_tensor(out=last[:, 0, :], in0=last[:, 0, :], in1=folded[:], op=ADD)
-            nc.vector.tensor_tensor(out=last[:, 1, :], in0=last[:, 1, :], in1=before[:, 1, :], op=ADD)
             result = totals.tile([P, CH], F32)
             halves = [slice(0, CH // 2), slice(CH // 2, CH)]
-            for half in halves:
-                nc.vector.tensor_tensor(out=last[:, 0, half], in0=last[:, 0, half], in1=last[:, 1, half], op=ADD)
+            for addend in (folded[:], last[:, 1, :]):
+                for half in halves:
+                    nc.vector.tensor_tensor(out=last[:, 0, half], in0=last[:, 0, half], in1=addend[:, half], op=ADD)
             for half in halves:
                 nc.vector.tensor_tensor(out=result[:, half], in0=sum_ps[:, half], in1=last[:, 0, half], op=ADD)
                 nc.sync.dma_start(out=out[NODES - P : NODES, half], in_=result[:, half])
@@ -357,5 +359,5 @@ def tile_treelstm_pa_kernel(tc, z_node, z_children, W_f_words, W_f_scales, U_f, 
         for child in range(PAIR):
             gate(ROUNDS - 1, child)
         weigh_shared(ROUNDS - 2)
-        sum_ps = sum_on_tensor([weighed_tiles[SUMMED_AT_END][:, 0, :], weighed_tiles[SUMMED_AT_END][:, 1, :], weighed_tiles[ROUNDS - 2][:, 0, :]])
+        sum_ps = sum_on_tensor([weighed_tiles[r][:, i, :] for r in range(SUMMED_AT_END, ROUNDS - 1) for i in range(PAIR)])
         finish(folded, sum_ps)

@@ -23,7 +23,7 @@ ROUNDS_PER_BLOCK = CHILDREN // PAIR
 ROUNDS = (NODES // P) * ROUNDS_PER_BLOCK
 AHEAD = 3
 IN_PIECES = 2
-GPSIMD_COLUMNS = 480
+GPSIMD_COLUMNS = 448
 
 def biased_by_tensor(r, i):
     return r >= ROUNDS - 2 and i == 0

@@ -23,7 +23,7 @@ ROUNDS_PER_BLOCK = CHILDREN // PAIR
 ROUNDS = (NODES // P) * ROUNDS_PER_BLOCK
 AHEAD = 3
 IN_PIECES = 2
-GPSIMD_COLUMNS = 448
+GPSIMD_COLUMNS = 432
 
 def biased_by_tensor(r, i):
     return r >= ROUNDS - 2 and i == 0

from contextlib import ExitStack

import concourse.mybir as mybir
from concourse.masks import make_identity

F32 = mybir.dt.float32
BF16 = mybir.dt.bfloat16
I32 = mybir.dt.int32
U32 = mybir.dt.uint32
U8 = mybir.dt.uint8
FP8X4 = mybir.dt.float8_e4m3fn_x4
FP4X4 = mybir.dt.float4_e2m1fn_x4
ADD = mybir.AluOpType.add
MULT = mybir.AluOpType.mult
SIGMOID = mybir.ActivationFunctionType.Sigmoid

P = 128
NODES, CHILDREN, SIZE, CH = 256, 16, 1024, 512
PASSES = SIZE // (4 * P)
K_TILES = CH // P
PAIR = 2
ROUNDS_PER_BLOCK = CHILDREN // PAIR
ROUNDS = (NODES // P) * ROUNDS_PER_BLOCK
AHEAD = 3
IN_PIECES = 2
GPSIMD_COLUMNS = 432

def biased_by_tensor(r, i):
    return r >= ROUNDS - 2 and i == 0


SUMMED_AT_END = ROUNDS - 3

FLOPS = 2 * NODES * CHILDREN * CH * (SIZE + CH)


def tile_treelstm_pa_kernel(tc, z_node, z_children, W_f_words, W_f_scales, U_f, b_f, out):
    nc = tc.nc
    with ExitStack() as stack:
        consts = stack.enter_context(tc.tile_pool(name="consts", bufs=1))
        z_pool = stack.enter_context(tc.tile_pool(name="z_pool", bufs=AHEAD + 1))
        c_pool = stack.enter_context(tc.tile_pool(name="c_pool", bufs=AHEAD + 4))
        work = stack.enter_context(tc.tile_pool(name="work", bufs=3))
        totals = stack.enter_context(tc.tile_pool(name="totals", bufs=2))
        psum_z = stack.enter_context(tc.psum_pool(name="psum_z", bufs=PAIR))
        psum_h = stack.enter_context(tc.psum_pool(name="psum_h", bufs=PAIR))
        psum_plain = stack.enter_context(tc.psum_pool(name="psum_plain", bufs=PAIR))
        psum_mx = stack.enter_context(tc.psum_pool(name="psum_mx", bufs=PAIR))
        stack.enter_context(tc.manual_schedule())

        z_tiles, c_tiles, zT_banks, hT_banks = {}, {}, {}, {}
        grouped_tiles, hT_tiles, code_tiles, plane_tiles = {}, {}, {}, {}
        plain_banks, mx_banks, pre_tiles, gate_tiles, total_tiles, weighed_tiles = {}, {}, {}, {}, {}, {}

        def load_hidden(r):
            nodes = slice((r // ROUNDS_PER_BLOCK) * P, (r // ROUNDS_PER_BLOCK + 1) * P)
            children = slice((r % ROUNDS_PER_BLOCK) * PAIR, (r % ROUNDS_PER_BLOCK + 1) * PAIR)
            c_sb = c_pool.tile([P, PAIR, SIZE], BF16)
            nc.sync.dma_start(out=c_sb[:, :, 0:CH], in_=z_children[nodes, children, 0:CH])
            c_tiles[r] = c_sb

        def load(r):
            nodes = slice((r // ROUNDS_PER_BLOCK) * P, (r // ROUNDS_PER_BLOCK + 1) * P)
            children = slice((r % ROUNDS_PER_BLOCK) * PAIR, (r % ROUNDS_PER_BLOCK + 1) * PAIR)
            z_sb = z_pool.tile([P, PAIR, SIZE], BF16)
            if r < IN_PIECES:
                for i in range(PAIR):
                    nc.sync.dma_start(out=z_sb[:, i, :], in_=z_node[nodes, children.start + i, :])
                    if r > 0 and i == 0:
                        load_hidden(r)
            else:
                c_sb = c_pool.tile([P, PAIR, SIZE], BF16)
                nc.sync.dma_start(out=z_sb[:], in_=z_node[nodes, children, :])
                nc.sync.dma_start(out=c_sb[:], in_=z_children[nodes, children, :])
                c_tiles[r] = c_sb
            z_tiles[r] = z_sb

        def load_cells(r):
            nodes = slice((r // ROUNDS_PER_BLOCK) * P, (r // ROUNDS_PER_BLOCK + 1) * P)
            children = slice((r % ROUNDS_PER_BLOCK) * PAIR, (r % ROUNDS_PER_BLOCK + 1) * PAIR)
            nc.sync.dma_start(out=c_tiles[r][:, :, CH:SIZE], in_=z_children[nodes, children, CH:SIZE])

        ones = consts.tile([P, P], BF16)
        nc.vector.memset(ones[:], 1.0)
        idle_columns = consts.tile([P, CH], BF16)
        nc.vector.memset(idle_columns[:], 0.0)
        idle_ps = psum_plain.tile([P, CH], F32, tag="plain_ps")

        def keep_clock(count):
            for k in range(count):
                nc.tensor.matmul(out=idle_ps[:], lhsT=ones[:], rhs=idle_columns[:], start=True, stop=True)

        keep_clock(3)

        load_hidden(0)
        u_sb = consts.tile([P, CH // P, CH], BF16)
        for half in range(2):
            nc.sync.dma_start(out=u_sb[:, 2 * half : 2 * half + 2, :], in_=U_f.rearrange("(a p) k -> p a k", p=P)[:, 2 * half : 2 * half + 2, :])
        ident = consts.tile([P, P], F32)
        make_identity(nc, ident[:])

        bias_row = consts.tile([P, CH], BF16)
        nc.vector.memset(bias_row[:], 0.0)

        warm = consts.tile([P, 1], F32)
        nc.vector.memset(warm[:], 0.0)
        nc.scalar.activation(out=warm[:], in_=warm[:], func=SIGMOID)

        w_planes = consts.tile([P, PASSES, CH], U8, align_bytes=64)
        nc.vector.memset(w_planes[:].bitcast(I32), 0)

        nc.sync.dma_start(out=bias_row[0:1, :], in_=b_f.rearrange("(o n) -> o n", o=1))
        load(0)
        load(1)
        w_words = consts.tile([P, PASSES, 2 * CH], U8, align_bytes=64)
        nc.sync.dma_start(out=w_words[:].bitcast(I32), in_=W_f_words.bitcast(I32).rearrange("g p n -> p g n"))
        for quadrant in range(4):
            nc.sync.dma_start(
                out=w_planes[32 * quadrant : 32 * quadrant + 4].bitcast(I32),
                in_=W_f_scales.bitcast(I32)[:, 4 * quadrant : 4 * quadrant + 4, :].rearrange("g q n -> q g n"),
            )
        for r in range(2, AHEAD):
            load(r)

        uT = consts.tile([P, 2, 2, CH], BF16)
        bias = consts.tile([P, CH], F32)

        def spread_bias():
            bias_ps = psum_mx.tile([P, CH], F32, tag="mx_ps")
            nc.tensor.matmul(out=bias_ps[:], lhsT=ones[:], rhs=bias_row[:], start=True, stop=True)
            nc.vector.tensor_copy(out=bias[:], in_=bias_ps[:])

        def prepare_plain_operands():
            for half in range(2):
                if half == 0:
                    uT_ps = psum_mx.tile([P, 2, 2, P], F32, tag="mx_ps")
                else:
                    uT_ps = psum_plain.tile([P, 2, 2, P], F32, tag="plain_ps")
                for a in range(2):
                    for u in range(2):
                        nc.tensor.transpose(uT_ps[:, u, a, :], u_sb[:, 2 * half + a, :].bitcast(F32)[:, P * u : P * (u + 1)], ident[:])
                columns = slice(half * CH // 2, (half + 1) * CH // 2)
                halves = uT_ps[:].rearrange("p u a c -> p (u a c)").bitcast(BF16).rearrange("p (u c e) -> p u e c", u=2, e=2)
                if half == 0:
                    nc.vector.tensor_copy(out=uT[:, :, :, columns], in_=halves)
                else:
                    nc.scalar.copy(out=uT[:, :, :, columns], in_=halves)

        def live(r):
            return 0 <= r < ROUNDS

        def open_banks(r, i):
            zT_ps = psum_z.tile([P, PASSES, 2, P], F32)
            hT_ps = psum_h.tile([P, 2, P], F32)
            zT_banks[r, i], hT_banks[r, i] = zT_ps, hT_ps

        def transpose_z(r, i, q):
            g, u = divmod(q, 2)
            words = z_tiles[r][:, i, :].bitcast(F32)
            nc.tensor.transpose(zT_banks[r, i][:, g, u, :], words[:, 2 * P * g + u : 2 * P * (g + 1) : 2], ident[:])

        def transpose_h(r, i, u):
            nc.tensor.transpose(hT_banks[r, i][:, u, :], c_tiles[r][:, i, 0:CH].bitcast(F32)[:, P * u : P * (u + 1)], ident[:])

        def first_transposes():
            for i in range(PAIR):
                open_banks(0, i)
                for u in range(2):
                    transpose_h(0, i, u)
                evacuate_h(0, i)
            keep_clock(1)
            prepare_plain_operands()
            keep_clock(1)
            for i in range(PAIR):
                for q in range(2 * PASSES):
                    transpose_z(0, i, q)
                evacuate_z(0, i)
                if i == 0:
                    spread_bias()

        def plain_and_transposes(s, i):
            if live(s - 1):
                plain_ps = psum_plain.tile([P, CH], F32)
                plain_banks[s - 1, i] = plain_ps
            if live(s):
                open_banks(s, i)

            bias_first = live(s - 1) and biased_by_tensor(s - 1, i)
            if bias_first:
                nc.tensor.matmul(out=plain_ps[:], lhsT=ones[:], rhs=bias_row[:], start=True, stop=False)
            for t in range(K_TILES):
                if live(s - 1):
                    nc.tensor.matmul(
                        out=plain_ps[:],
                        lhsT=hT_tiles[s - 1, i][:, t // 2, t % 2, :],
                        rhs=uT[:, t // 2, t % 2, :],
                        start=(t == 0 and not bias_first),
                        stop=(t == K_TILES - 1),
                    )
                if live(s):
                    if t < K_TILES - 1 or i == 0:
                        transpose_z(s, i, t)
                    if t < 2:
                        transpose_h(s, i, t)
                    if t == K_TILES - 2 and i == 1:
                        transpose_z(s, i, t + 1)

        def evacuate_z(r, i):
            if i == 0:
                pair_grouped = work.tile([P, PAIR, PASSES, P, 4], BF16, align_bytes=64, name="pair_grouped")
                grouped_tiles[r] = pair_grouped
            grouped, words = grouped_tiles[r][:, i].bitcast(F32), zT_banks[r, i][:].rearrange("p g u m -> p g m u")
            if (r, i) == (0, 0):
                nc.vector.tensor_copy(out=grouped, in_=words)
            else:
                nc.scalar.copy(out=grouped, in_=words)

        def evacuate_h(r, i):
            hT = work.tile([P, 2, 2, P], BF16, bufs=3 * PAIR)
            halves = hT_banks[r, i][:].rearrange("p u m -> p (u m)").bitcast(BF16).rearrange("p (u m e) -> p u e m", u=2, e=2)
            nc.scalar.copy(out=hT[:], in_=halves)
            hT_tiles[r, i] = hT

        def quantise(r):
            codes = work.tile([P, PAIR, PASSES, P], U32, align_bytes=64)
            planes = work.tile([P, PAIR, PASSES, P], U8, align_bytes=64)
            nc.vector.quantize_mx(
                out=codes[:].rearrange("p i g m -> p (i g m)").bitcast(FP8X4),
                scales=planes[:].rearrange("p i g m -> p (i g m)"),
                in_=grouped_tiles[r][:].rearrange("p i g m t -> p (i g m t)"),
            )
            code_tiles[r], plane_tiles[r] = codes, planes

        def mx(r):
            mx_banks[r] = []
            for i in range(PAIR):
                mx_ps = psum_mx.tile([P, CH], F32)
                for g in range(PASSES):
                    nc.tensor.matmul_mx(
                        out=mx_ps[:],
                        lhsT=code_tiles[r][:, i, g, :].bitcast(FP8X4),
                        lhsT_scale=plane_tiles[r][:, i, g, :],
                        rhs=w_words[:, g, :].bitcast(FP4X4),
                        rhs_scale=w_planes[:, g, :],
                        start=(g == 0),
                        stop=(g == PASSES - 1),
                    )
                mx_banks[r].append(mx_ps)

        def add_bias(r, i):
            if i == 0:
                pre = work.tile([P, PAIR, CH], F32)
                pre_tiles[r] = pre
            if biased_by_tensor(r, i):
                nc.scalar.copy(out=pre_tiles[r][:, i, :], in_=plain_banks[r, i][:])
            else:
                nc.vector.tensor_tensor(out=pre_tiles[r][:, i, :], in0=plain_banks[r, i][:], in1=bias[:], op=ADD)

        def add_mx(r):
            for i in range(PAIR):
                nc.vector.tensor_tensor(out=pre_tiles[r][:, i, :], in0=mx_banks[r][i][:], in1=pre_tiles[r][:, i, :], op=ADD)

        def gate(r, i):
            if i == 0:
                gates = work.tile([P, PAIR, CH], F32)
                gate_tiles[r] = gates
            nc.scalar.activation(out=gate_tiles[r][:, i, :], in_=pre_tiles[r][:, i, :], func=SIGMOID)

        def products(r, engine, out, columns=slice(0, CH)):
            cells = slice(CH + columns.start, CH + columns.stop)
            engine.tensor_tensor(out=out[:, :, columns], in0=gate_tiles[r][:, :, columns], in1=c_tiles[r][:, :, cells], op=MULT)
            weighed_tiles[r] = out

        def weigh(r):
            weighed = work.tile([P, PAIR, CH], F32, name="shared_weighed", bufs=1)
            products(r, nc.gpsimd, weighed, slice(0, GPSIMD_COLUMNS))
            products(r, nc.vector, weighed, slice(GPSIMD_COLUMNS, CH))

        def weigh_at_end(r):
            weighed = work.tile([P, PAIR, CH], F32, name="weighed")
            products(r, nc.vector, weighed)

        def add_up(r):
            block, turn = divmod(r, ROUNDS_PER_BLOCK)
            if turn == 0:
                total = totals.tile([P, PAIR, CH], F32)
                total_tiles[block] = total
                products(r, nc.vector, total)
            else:
                total = total_tiles[block]
                nc.vector.tensor_tensor(out=total[:], in0=total[:], in1=weighed_tiles[r][:], op=ADD)

        def fold_total(block):
            total = total_tiles[block]
            folded = totals.tile([P, CH], F32)
            nc.gpsimd.tensor_tensor(out=folded[:], in0=total[:, 0, :], in1=total[:, 1, :], op=ADD)
            return folded

        def weigh_shared(r):
            weighed = work.tile([P, PAIR, CH], F32, name="weighed")
            for i, engine in enumerate((nc.gpsimd, nc.vector)):
                engine.tensor_tensor(out=weighed[:, i, :], in0=gate_tiles[r][:, i, :], in1=c_tiles[r][:, i, CH:SIZE], op=MULT)
            weighed_tiles[r] = weighed

        def sum_on_tensor(tiles):
            sum_ps = psum_plain.tile([P, CH], F32, tag="plain_ps")
            for k, tile in enumerate(tiles):
                nc.tensor.matmul(out=sum_ps[:], lhsT=ident[:], rhs=tile, start=(k == 0), stop=(k == len(tiles) - 1))
            return sum_ps

        def finish(folded, sum_ps):
            r = ROUNDS - 1
            last = work.tile([P, PAIR, CH], F32, name="weighed")
            for i in range(PAIR):
                nc.vector.tensor_tensor(out=last[:, i, :], in0=gate_tiles[r][:, i, :], in1=c_tiles[r][:, i, CH:SIZE], op=MULT)
            result = totals.tile([P, CH], F32)
            halves = [slice(0, CH // 2), slice(CH // 2, CH)]
            for addend in (folded[:], last[:, 1, :]):
                for half in halves:
                    nc.vector.tensor_tensor(out=last[:, 0, half], in0=last[:, 0, half], in1=addend[:, half], op=ADD)
            for half in halves:
                nc.vector.tensor_tensor(out=result[:, half], in0=sum_ps[:, half], in1=last[:, 0, half], op=ADD)
                nc.sync.dma_start(out=out[NODES - P : NODES, half], in_=result[:, half])

        def run(stage, r, *which):
            if live(r):
                stage(r, *which)

        for s in range(ROUNDS + 1):
            run(load, s + AHEAD)
            run(quantise, s - 1)
            if live(s - 3):
                block, turn = divmod(s - 3, ROUNDS_PER_BLOCK)
                if turn == 0 and block > 0:
                    nc.sync.dma_start(out=out[(block - 1) * P : block * P, :], in_=fold_total(block - 1)[:])
                elif s - 3 == SUMMED_AT_END:
                    folded = fold_total(block)
                elif turn > 0:
                    weigh(s - 3)
            run(add_mx, s - 2)
            if s - 3 == SUMMED_AT_END:
                weigh_at_end(s - 3)
            if s == 0:
                first_transposes()
            else:
                for i in range(PAIR):
                    plain_and_transposes(s, i)
                    run(evacuate_z, s, i)
                    run(add_bias, s - 1, i)
                    run(evacuate_h, s, i)
            for child in range(PAIR):
                run(gate, s - 2, child)
            if s - 3 < SUMMED_AT_END:
                run(add_up, s - 3)
            if s < IN_PIECES:
                load_cells(s)
            run(mx, s - 1)
        add_mx(ROUNDS - 1)
        for child in range(PAIR):
            gate(ROUNDS - 1, child)
        weigh_shared(ROUNDS - 2)
        sum_ps = sum_on_tensor([weighed_tiles[r][:, i, :] for r in range(SUMMED_AT_END, ROUNDS - 1) for i in range(PAIR)])
        finish(folded, sum_ps)
